import numpy as np
import ml_dtypes


def mxq(x, axis, fmt="e4m3"):
    dtype, down = {"e4m3": (ml_dtypes.float8_e4m3fn, 7), "e5m2": (ml_dtypes.float8_e5m2, 14)}[fmt]
    v = np.moveaxis(np.asarray(x, np.float32).astype(ml_dtypes.bfloat16).astype(np.float64), axis, -1)
    blocks = v.reshape(v.shape[:-1] + (-1, 32))
    amax = np.abs(blocks).max(-1, keepdims=True)
    byte = np.maximum(np.where(amax > 0, np.frexp(amax)[1] - 1 + 127, 0) - down, 1)
    scale = np.exp2(byte - 127.0)
    codes = (blocks / scale).astype(np.float32).astype(dtype).astype(np.float64)
    return np.moveaxis((codes * scale).reshape(v.shape), -1, axis)


WIDE = False


def mx_kscale(k):
    if not WIDE:
        return np.ones(k)
    levels = np.array([10, -10, 5, -5, 0])
    a = np.random.permutation(np.resize(levels, k // 512 * 4)).reshape(k // 512, 4)
    idx = np.arange(k)
    return np.exp2(a[idx // 512, idx % 128 // 32])


BF16 = ml_dtypes.bfloat16


def bf(x):
    return np.asarray(x, np.float32).astype(BF16)


def f64(x):
    return np.asarray(x).astype(np.float64)


B, D_IN, D_H, C = 8192, 512, 512, 128
TAU, T1, T2 = 0.5, 3, 3
G, GB = 3.0, 3.0


def inv_apprx(v, t, m):
    a = 2.0 - (2.0 / m) * v
    b = 1.0 - (2.0 / m) * v
    for _ in range(t):
        b = b * b
        a = a * (1.0 + b)
    return (2.0 / m) * a


def comp_max_tau(p, tau, t1, t2):
    res = np.concatenate([p, np.full((p.shape[0], 1), tau)], axis=1)
    for i in range(t1):
        res = res * res
        sum_res = res.sum(axis=1)
        m = (2.0 + tau * tau) if i == 0 else 2.0
        res = res * inv_apprx(sum_res, t2, m)[:, None]
    return res[:, -1]


def softmax(z):
    e = np.exp(z - z.max(-1, keepdims=True))
    return e / e.sum(-1, keepdims=True)


def mlp(xq, W1, b1, W2, b2):
    h = np.maximum((xq @ mxq(f64(W1), 0, "e4m3")) + f64(b1), 0.0)
    return softmax((mxq(h, 1, "e4m3") @ mxq(f64(W2), 0, "e4m3")) + f64(b2))


def setup_inputs():
    s, t = mx_kscale(D_IN), mx_kscale(D_H)
    return {"x": bf(np.random.standard_normal((B, D_IN)) * s),
            "W1o": bf(np.random.standard_normal((D_IN, D_H)) / np.sqrt(D_IN) / s[:, None] * t),
            "b1o": bf(np.random.standard_normal(D_H) * 0.2 * t),
            "W2o": bf(np.random.standard_normal((D_H, C)) * G / np.sqrt(D_H) / t[:, None]),
            "b2o": bf(np.random.standard_normal(C) * GB),
            "W1f": bf(np.random.standard_normal((D_IN, D_H)) / np.sqrt(D_IN) / s[:, None] * t),
            "b1f": bf(np.random.standard_normal(D_H) * 0.2 * t),
            "W2f": bf(np.random.standard_normal((D_H, C)) * G / np.sqrt(D_H) / t[:, None]),
            "b2f": bf(np.random.standard_normal(C) * GB)}


def reference(x, W1o, b1o, W2o, b2o, W1f, b1f, W2f, b2f):
    xq = mxq(f64(x), 1, "e4m3")
    x1 = mlp(xq, W1o, b1o, W2o, b2o)
    x2 = mlp(xq, W1f, b1f, W2f, b2f)
    cond_in = comp_max_tau(x1, TAU, T1, T2)
    return x1 * (1.0 - cond_in[:, None]) + x2 * cond_in[:, None]

@@ -1,0 +1,290 @@
+from contextlib import ExitStack
+
+import concourse.mybir as mybir
+from concourse.masks import make_identity
+
+F32 = mybir.dt.float32
+BF16 = mybir.dt.bfloat16
+U32 = mybir.dt.uint32
+U8 = mybir.dt.uint8
+FP8X4 = mybir.dt.float8_e4m3fn_x4
+ACT = mybir.ActivationFunctionType
+ALU = mybir.AluOpType
+AXIS = mybir.AxisListType
+
+P = 128
+PACK = 4
+ROWS, D_IN, D_H, CLASSES = 8192, 512, 512, 128
+TILES = ROWS // P
+GROUP_TILES = 4
+GROUP_ROWS = GROUP_TILES * P
+GROUPS = TILES // GROUP_TILES
+WORDS = D_IN // 2
+TAU = 0.5
+SERIES_STEPS = 3
+
+FLOPS = 2 * (2 * ROWS * D_IN * D_H + 2 * ROWS * D_H * CLASSES)
+
+
+def quantise(nc, grouped, codes, scales):
+    nc.vector.quantize_mx(out=codes.bitcast(FP8X4), scales=scales, in_=grouped)
+
+
+def mx_pass(nc, acc, stationary, moving):
+    nc.tensor.matmul_mx(
+        out=acc,
+        lhsT=stationary[0].bitcast(FP8X4),
+        lhsT_scale=stationary[1],
+        rhs=moving[0].bitcast(FP8X4),
+        rhs_scale=moving[1],
+        start=True,
+        stop=True,
+    )
+
+
+def load_network(nc, keep, setup, net, w1, b1, w2, b2):
+    w1_raw = setup.tile([P, PACK, D_H], BF16, name="w1_raw_" + net)
+    nc.sync.dma_start(
+        out=w1_raw[:].rearrange("p (u e) h -> p u e h", u=2),
+        in_=w1.rearrange("(u p e) h -> p u e h", u=2, e=2),
+    )
+    w1_grouped = setup.tile([P, D_H, PACK], BF16, name="w1_grouped_" + net, align_bytes=64)
+    nc.vector.tensor_copy(
+        out=w1_grouped[:].rearrange("p (t m) j -> p t m j", t=PACK),
+        in_=w1_raw[:].rearrange("p j (m t) -> p t m j", t=PACK),
+    )
+    w1_codes = keep.tile([P, D_H], U32, name="w1_codes_" + net, align_bytes=64)
+    w1_scales = keep.tile([P, D_H], U8, name="w1_scales_" + net, align_bytes=64)
+    quantise(nc, w1_grouped[:].rearrange("p c j -> p (c j)"), w1_codes[:], w1_scales[:])
+
+    b1_raw = setup.tile([P, PACK], BF16, name="b1_raw_" + net)
+    nc.scalar.dma_start(out=b1_raw[:], in_=b1.rearrange("(p t) -> p t", t=PACK))
+    b1_cols = keep.tile([P, PACK], F32, name="b1_cols_" + net)
+    nc.vector.tensor_copy(out=b1_cols[:], in_=b1_raw[:])
+
+    w2_raw = setup.tile([P, PACK, CLASSES], BF16, name="w2_raw_" + net)
+    nc.scalar.dma_start(out=w2_raw[:], in_=w2.rearrange("(p t) c -> p t c", t=PACK))
+    w2_grouped = setup.tile([P, CLASSES, PACK], BF16, name="w2_grouped_" + net, align_bytes=64)
+    nc.vector.tensor_copy(out=w2_grouped[:], in_=w2_raw[:].rearrange("p t c -> p c t"))
+    w2_codes = keep.tile([P, CLASSES], U32, name="w2_codes_" + net, align_bytes=64)
+    w2_scales = keep.tile([P, CLASSES], U8, name="w2_scales_" + net, align_bytes=64)
+    quantise(nc, w2_grouped[:].rearrange("p c t -> p (c t)"), w2_codes[:], w2_scales[:])
+
+    b2_raw = setup.tile([P, CLASSES], BF16, name="b2_raw_" + net)
+    nc.scalar.dma_start(out=b2_raw[:], in_=b2.partition_broadcast(P))
+    b2_rows = keep.tile([P, CLASSES], F32, name="b2_rows_" + net)
+    nc.vector.tensor_copy(out=b2_rows[:], in_=b2_raw[:])
+
+    return {
+        "w1": (w1_codes, w1_scales),
+        "b1": b1_cols,
+        "w2": (w2_codes, w2_scales),
+        "b2": b2_rows,
+    }
+
+
+def gp_affine(nc, out, in_, mul, add):
+    nc.gpsimd.tensor_scalar(out=out, in0=in_, scalar1=mul, scalar2=add, op0=ALU.mult, op1=ALU.add)
+
+
+def gp_mul(nc, out, in0, in1):
+    nc.gpsimd.tensor_tensor(out=out, in0=in0, in1=in1, op=ALU.mult)
+
+
+def inverse_series(nc, gate, total, m, name):
+    b = gate.tile([P, TILES], F32, name="b_" + name)
+    a = gate.tile([P, TILES], F32, name="a_" + name)
+    one_plus_b = gate.tile([P, TILES], F32, name="one_plus_b_" + name)
+    gp_affine(nc, b[:], total, -2.0 / m, 1.0)
+    gp_affine(nc, a[:], b[:], 1.0, 1.0)
+    for step in range(SERIES_STEPS):
+        gp_mul(nc, b[:], b[:], b[:])
+        gp_affine(nc, one_plus_b[:], b[:], 1.0, 1.0)
+        gp_mul(nc, a[:], a[:], one_plus_b[:])
+    return a
+
+
+def gate_weights(nc, gate, sums):
+    def new(name):
+        return gate.tile([P, TILES], F32, name=name)
+
+    recip1, recip2, recip4, recip8 = new("recip1"), new("recip2"), new("recip4"), new("recip8")
+    nc.vector.reciprocal(out=recip1[:], in_=sums["e1"][:])
+    gp_mul(nc, recip2[:], recip1[:], recip1[:])
+    gp_mul(nc, recip4[:], recip2[:], recip2[:])
+    gp_mul(nc, recip8[:], recip4[:], recip4[:])
+
+    total0, inv0, scale1 = new("total0"), new("inv0"), new("scale1")
+    gp_mul(nc, total0[:], sums["e2"][:], recip2[:])
+    gp_affine(nc, total0[:], total0[:], 1.0, TAU**2)
+    m0 = 2.0 + TAU**2
+    a0 = inverse_series(nc, gate, total0[:], m0, "0")
+    gp_affine(nc, inv0[:], a0[:], 2.0 / m0, 0.0)
+    gp_mul(nc, scale1[:], inv0[:], inv0[:])
+
+    total1, scale2 = new("total1"), new("scale2")
+    gp_mul(nc, total1[:], sums["e4"][:], recip4[:])
+    gp_affine(nc, total1[:], total1[:], 1.0, TAU**4)
+    gp_mul(nc, total1[:], total1[:], scale1[:])
+    a1 = inverse_series(nc, gate, total1[:], 2.0, "1")
+    gp_mul(nc, scale2[:], scale1[:], a1[:])
+    gp_mul(nc, scale2[:], scale2[:], scale2[:])
+
+    total2, cond, alpha = new("total2"), new("cond"), new("alpha")
+    gp_mul(nc, total2[:], sums["e8"][:], recip8[:])
+    gp_affine(nc, total2[:], total2[:], 1.0, TAU**8)
+    gp_mul(nc, total2[:], total2[:], scale2[:])
+    a2 = inverse_series(nc, gate, total2[:], 2.0, "2")
+    gp_mul(nc, cond[:], scale2[:], a2[:])
+    gp_affine(nc, cond[:], cond[:], TAU**8, 0.0)
+
+    gp_affine(nc, alpha[:], cond[:], -1.0, 1.0)
+    gp_mul(nc, alpha[:], alpha[:], recip1[:])
+    return cond, alpha
+
+
+def tile_combnethe_pa_t_kernel(tc, x, W1o, b1o, W2o, b2o, W1f, b1f, W2f, b2f, out):
+    nc = tc.nc
+    x_rows = x.rearrange("(p j) k -> p j k", j=TILES)
+    out_rows = out.rearrange("(p j) c -> p j c", j=TILES)
+
+    with ExitStack() as pools:
+        keep = pools.enter_context(tc.tile_pool(name="keep", bufs=1))
+        x_pool = pools.enter_context(tc.tile_pool(name="x_pool", bufs=3))
+
+        def load_x(g):
+            x_sb = x_pool.tile([P, GROUP_TILES * D_IN], BF16, name="x_sb")
+            nc.sync.dma_start(
+                out=x_sb[:].rearrange("p (j k) -> p j k", j=GROUP_TILES),
+                in_=x_rows[:, g * GROUP_TILES : (g + 1) * GROUP_TILES, :],
+            )
+            return x_sb
+
+        x_next = load_x(0)
+
+        identity = keep.tile([P, P], F32, name="identity")
+        make_identity(nc, identity[:])
+        with tc.tile_pool(name="setup", bufs=1) as setup:
+            net_o = load_network(nc, keep, setup, "o", W1o, b1o, W2o, b2o)
+            net_f = load_network(nc, keep, setup, "f", W1f, b1f, W2f, b2f)
+
+        work = pools.enter_context(tc.tile_pool(name="work", bufs=2))
+        small = pools.enter_context(tc.tile_pool(name="small", bufs=4))
+        gate = pools.enter_context(tc.tile_pool(name="gate", bufs=1))
+        psum_x = pools.enter_context(tc.psum_pool(name="psum_x", bufs=2))
+        psum_z = pools.enter_context(tc.psum_pool(name="psum_z", bufs=4))
+        psum_l = pools.enter_context(tc.psum_pool(name="psum_l", bufs=2))
+
+        def quantise_x(g, x_sb):
+            x_words = x_sb[:].bitcast(F32)
+            x_grouped = work.tile([P, GROUP_ROWS * PACK], BF16, name="x_grouped", align_bytes=64)
+            grouped_words = x_grouped[:].bitcast(F32)
+            for half in range(2):
+                x_t = psum_x.tile([P, 2, 2, P], F32, name="x_t")
+                for jj in range(2):
+                    for u in range(2):
+                        first = (2 * half + jj) * WORDS + u * P
+                        nc.tensor.transpose(x_t[:, jj, u, :], x_words[:, first : first + P], identity[:])
+                nc.vector.tensor_copy(
+                    out=grouped_words[:, half * 2 * WORDS : (half + 1) * 2 * WORDS].rearrange(
+                        "p (j r u) -> p j r u", j=2, u=2
+                    ),
+                    in_=x_t[:].rearrange("p j u r -> p j r u"),
+                )
+            codes = keep.tile([P, GROUP_ROWS], U32, name="x_codes_%d" % g, align_bytes=64)
+            scales = keep.tile([P, GROUP_ROWS], U8, name="x_scales_%d" % g, align_bytes=64)
+            quantise(nc, x_grouped[:], codes[:], scales[:])
+            return codes, scales
+
+        def softmax_numerators(net, x_q, e, e_sum):
+            w1_codes, w1_scales = net["w1"]
+            planes = work.tile([P, PACK, GROUP_ROWS], BF16, name="planes")
+            for t in range(PACK):
+                z = psum_z.tile([P, GROUP_ROWS], F32, name="z")
+                cols = slice(t * P, (t + 1) * P)
+                mx_pass(nc, z[:], (w1_codes[:, cols], w1_scales[:, cols]), (x_q[0][:], x_q[1][:]))
+                nc.scalar.activation(
+                    out=planes[:, t, :], in_=z[:], func=ACT.Relu, bias=net["b1"][:, t : t + 1], scale=1.0
+                )
+            h_grouped = work.tile([P, GROUP_ROWS, PACK], BF16, name="h_grouped", align_bytes=64)
+            nc.vector.tensor_copy(
+                out=h_grouped[:].rearrange("p (c i) t -> p c t i", i=4),
+                in_=planes[:].rearrange("p t (c i) -> p c t i", i=4),
+            )
+            h_codes = work.tile([P, GROUP_ROWS], U32, name="h_codes", align_bytes=64)
+            h_scales = work.tile([P, GROUP_ROWS], U8, name="h_scales", align_bytes=64)
+            quantise(nc, h_grouped[:].rearrange("p r t -> p (r t)"), h_codes[:], h_scales[:])
+
+            acc = psum_l.tile([P, GROUP_TILES, CLASSES], F32, name="acc")
+            for j in range(GROUP_TILES):
+                cols = slice(j * P, (j + 1) * P)
+                mx_pass(nc, acc[:, j, :], (h_codes[:, cols], h_scales[:, cols]), (net["w2"][0][:], net["w2"][1][:]))
+            logits = work.tile([P, GROUP_TILES, CLASSES], F32, name="logits")
+            nc.vector.tensor_tensor(
+                out=logits[:],
+                in0=acc[:],
+                in1=net["b2"][:].unsqueeze(1).to_broadcast([P, GROUP_TILES, CLASSES]),
+                op=ALU.add,
+            )
+            neg_max = small.tile([P, GROUP_TILES], F32, name="neg_max")
+            nc.vector.tensor_reduce(out=neg_max[:], in_=logits[:], axis=AXIS.X, op=ALU.max, negate=True)
+            for j in range(GROUP_TILES):
+                nc.scalar.activation(
+                    out=e[:, j, :],
+                    in_=logits[:, j, :],
+                    func=ACT.Exp,
+                    bias=neg_max[:, j : j + 1],
+                    scale=1.0,
+                    accum_out=e_sum[:, j : j + 1],
+                )
+
+        sums = {}
+        for power in ("e1", "e2", "e4", "e8"):
+            sums[power] = gate.tile([P, TILES], F32, name="sum_" + power)
+        x_quantised = []
+        e_o = []
+        for g in range(GROUPS):
+            x_sb = x_next
+            if g + 1 < GROUPS:
+                x_next = load_x(g + 1)
+            x_quantised.append(quantise_x(g, x_sb))
+            tiles = slice(g * GROUP_TILES, (g + 1) * GROUP_TILES)
+            e_o.append(keep.tile([P, GROUP_TILES, CLASSES], F32, name="e_o_%d" % g))
+            softmax_numerators(net_o, x_quantised[g], e_o[g], sums["e1"][:, tiles])
+            powers = work.tile([P, GROUP_TILES, CLASSES], F32, name="powers")
+            for power in ("e2", "e4", "e8"):
+                for j in range(GROUP_TILES):
+                    nc.scalar.activation(
+                        out=powers[:, j, :],
+                        in_=e_o[g][:, j, :] if power == "e2" else powers[:, j, :],
+                        func=ACT.Square,
+                        accum_out=sums[power][:, g * GROUP_TILES + j : g * GROUP_TILES + j + 1],
+                    )
+
+        cond, alpha = gate_weights(nc, gate, sums)
+
+        for g in range(GROUPS):
+            tiles = slice(g * GROUP_TILES, (g + 1) * GROUP_TILES)
+            e_f = keep.tile([P, GROUP_TILES, CLASSES], F32, name="e_f_%d" % g)
+            sum_f = small.tile([P, GROUP_TILES], F32, name="sum_f")
+            softmax_numerators(net_f, x_quantised[g], e_f, sum_f[:])
+            beta = small.tile([P, GROUP_TILES], F32, name="beta")
+            nc.vector.reciprocal(out=beta[:], in_=sum_f[:])
+            nc.vector.tensor_mul(out=beta[:], in0=beta[:], in1=cond[:, tiles])
+            for j in range(GROUP_TILES):
+                tile_index = g * GROUP_TILES + j
+                nc.scalar.activation(
+                    out=e_o[g][:, j, :],
+                    in_=e_o[g][:, j, :],
+                    func=ACT.Copy,
+                    scale=alpha[:, tile_index : tile_index + 1],
+                )
+                nc.vector.scalar_tensor_tensor(
+                    out=e_f[:, j, :],
+                    in0=e_f[:, j, :],
+                    scalar=beta[:, j : j + 1],
+                    in1=e_o[g][:, j, :],
+                    op0=ALU.mult,
+                    op1=ALU.add,
+                )
+            nc.sync.dma_start(out=out_rows[:, tiles, :], in_=e_f[:])

@@ -19,6 +19,8 @@ TILES = ROWS // P
 GROUP_TILES = 4
 GROUP_ROWS = GROUP_TILES * P
 GROUPS = TILES // GROUP_TILES
+HALF_GROUPS = GROUPS // 2
+HALF_TILES = TILES // 2
 WORDS = D_IN // 2
 TAU = 0.5
 SERIES_STEPS = 3
@@ -92,9 +94,9 @@ def gp_mul(nc, out, in0, in1):
 
 
 def inverse_series(nc, gate, total, m, name):
-    b = gate.tile([P, TILES], F32, name="b_" + name)
-    a = gate.tile([P, TILES], F32, name="a_" + name)
-    one_plus_b = gate.tile([P, TILES], F32, name="one_plus_b_" + name)
+    b = gate.tile([P, HALF_TILES], F32, name="b_" + name)
+    a = gate.tile([P, HALF_TILES], F32, name="a_" + name)
+    one_plus_b = gate.tile([P, HALF_TILES], F32, name="one_plus_b_" + name)
     gp_affine(nc, b[:], total, -2.0 / m, 1.0)
     gp_affine(nc, a[:], b[:], 1.0, 1.0)
     for step in range(SERIES_STEPS):
@@ -104,37 +106,40 @@ def inverse_series(nc, gate, total, m, name):
     return a
 
 
-def gate_weights(nc, gate, sums):
+def gate_weights(nc, gate, sums, half):
+    cols = slice(half * HALF_TILES, (half + 1) * HALF_TILES)
+    tag = "_%d" % half
+
     def new(name):
-        return gate.tile([P, TILES], F32, name=name)
+        return gate.tile([P, HALF_TILES], F32, name=name + tag)
 
     recip1, recip2, recip4, recip8 = new("recip1"), new("recip2"), new("recip4"), new("recip8")
-    nc.vector.reciprocal(out=recip1[:], in_=sums["e1"][:])
+    nc.vector.reciprocal(out=recip1[:], in_=sums["e1"][:, cols])
     gp_mul(nc, recip2[:], recip1[:], recip1[:])
     gp_mul(nc, recip4[:], recip2[:], recip2[:])
     gp_mul(nc, recip8[:], recip4[:], recip4[:])
 
     total0, inv0, scale1 = new("total0"), new("inv0"), new("scale1")
-    gp_mul(nc, total0[:], sums["e2"][:], recip2[:])
+    gp_mul(nc, total0[:], sums["e2"][:, cols], recip2[:])
     gp_affine(nc, total0[:], total0[:], 1.0, TAU**2)
     m0 = 2.0 + TAU**2
-    a0 = inverse_series(nc, gate, total0[:], m0, "0")
+    a0 = inverse_series(nc, gate, total0[:], m0, "0" + tag)
     gp_affine(nc, inv0[:], a0[:], 2.0 / m0, 0.0)
     gp_mul(nc, scale1[:], inv0[:], inv0[:])
 
     total1, scale2 = new("total1"), new("scale2")
-    gp_mul(nc, total1[:], sums["e4"][:], recip4[:])
+    gp_mul(nc, total1[:], sums["e4"][:, cols], recip4[:])
     gp_affine(nc, total1[:], total1[:], 1.0, TAU**4)
     gp_mul(nc, total1[:], total1[:], scale1[:])
-    a1 = inverse_series(nc, gate, total1[:], 2.0, "1")
+    a1 = inverse_series(nc, gate, total1[:], 2.0, "1" + tag)
     gp_mul(nc, scale2[:], scale1[:], a1[:])
     gp_mul(nc, scale2[:], scale2[:], scale2[:])
 
     total2, cond, alpha = new("total2"), new("cond"), new("alpha")
-    gp_mul(nc, total2[:], sums["e8"][:], recip8[:])
+    gp_mul(nc, total2[:], sums["e8"][:, cols], recip8[:])
     gp_affine(nc, total2[:], total2[:], 1.0, TAU**8)
     gp_mul(nc, total2[:], total2[:], scale2[:])
-    a2 = inverse_series(nc, gate, total2[:], 2.0, "2")
+    a2 = inverse_series(nc, gate, total2[:], 2.0, "2" + tag)
     gp_mul(nc, cond[:], scale2[:], a2[:])
     gp_affine(nc, cond[:], cond[:], TAU**8, 0.0)
 
@@ -168,7 +173,7 @@ def tile_combnethe_pa_t_kernel(tc, x, W1o, b1o, W2o, b2o, W1f, b1f, W2f, b2f, ou
             net_o = load_network(nc, keep, setup, "o", W1o, b1o, W2o, b2o)
             net_f = load_network(nc, keep, setup, "f", W1f, b1f, W2f, b2f)
 
-        work = pools.enter_context(tc.tile_pool(name="work", bufs=2))
+        work = pools.enter_context(tc.tile_pool(name="work", bufs=3))
         small = pools.enter_context(tc.tile_pool(name="small", bufs=4))
         gate = pools.enter_context(tc.tile_pool(name="gate", bufs=1))
         psum_x = pools.enter_context(tc.psum_pool(name="psum_x", bufs=2))
@@ -196,16 +201,20 @@ def tile_combnethe_pa_t_kernel(tc, x, W1o, b1o, W2o, b2o, W1f, b1f, W2f, b2f, ou
             quantise(nc, x_grouped[:], codes[:], scales[:])
             return codes, scales
 
-        def softmax_numerators(net, x_q, e, e_sum):
+        def softmax_numerators(net, x_q, e, e_sum, vector_planes):
             w1_codes, w1_scales = net["w1"]
             planes = work.tile([P, PACK, GROUP_ROWS], BF16, name="planes")
             for t in range(PACK):
                 z = psum_z.tile([P, GROUP_ROWS], F32, name="z")
                 cols = slice(t * P, (t + 1) * P)
                 mx_pass(nc, z[:], (w1_codes[:, cols], w1_scales[:, cols]), (x_q[0][:], x_q[1][:]))
-                nc.scalar.activation(
-                    out=planes[:, t, :], in_=z[:], func=ACT.Relu, bias=net["b1"][:, t : t + 1], scale=1.0
-                )
+                bias = net["b1"][:, t : t + 1]
+                if t < PACK - vector_planes:
+                    nc.scalar.activation(out=planes[:, t, :], in_=z[:], func=ACT.Relu, bias=bias, scale=1.0)
+                else:
+                    nc.vector.tensor_scalar(
+                        out=planes[:, t, :], in0=z[:], scalar1=bias, scalar2=0.0, op0=ALU.add, op1=ALU.max
+                    )
             h_grouped = work.tile([P, GROUP_ROWS, PACK], BF16, name="h_grouped", align_bytes=64)
             nc.vector.tensor_copy(
                 out=h_grouped[:].rearrange("p (c i) t -> p c t i", i=4),
@@ -243,6 +252,7 @@ def tile_combnethe_pa_t_kernel(tc, x, W1o, b1o, W2o, b2o, W1f, b1f, W2f, b2f, ou
             sums[power] = gate.tile([P, TILES], F32, name="sum_" + power)
         x_quantised = []
         e_o = []
+        cond = []
         for g in range(GROUPS):
             x_sb = x_next
             if g + 1 < GROUPS:
@@ -250,7 +260,7 @@ def tile_combnethe_pa_t_kernel(tc, x, W1o, b1o, W2o, b2o, W1f, b1f, W2f, b2f, ou
             x_quantised.append(quantise_x(g, x_sb))
             tiles = slice(g * GROUP_TILES, (g + 1) * GROUP_TILES)
             e_o.append(keep.tile([P, GROUP_TILES, CLASSES], F32, name="e_o_%d" % g))
-            softmax_numerators(net_o, x_quantised[g], e_o[g], sums["e1"][:, tiles])
+            softmax_numerators(net_o, x_quantised[g], e_o[g], sums["e1"][:, tiles], g % 2)
             powers = work.tile([P, GROUP_TILES, CLASSES], F32, name="powers")
             for power in ("e2", "e4", "e8"):
                 for j in range(GROUP_TILES):
@@ -260,25 +270,35 @@ def tile_combnethe_pa_t_kernel(tc, x, W1o, b1o, W2o, b2o, W1f, b1f, W2f, b2f, ou
                         func=ACT.Square,
                         accum_out=sums[power][:, g * GROUP_TILES + j : g * GROUP_TILES + j + 1],
                     )
+            if (g + 1) % HALF_GROUPS == 0:
+                half = g // HALF_GROUPS
+                cond_half, alpha = gate_weights(nc, gate, sums, half)
+                cond.append(cond_half)
+                for member in range(HALF_GROUPS):
+                    scaled = e_o[half * HALF_GROUPS + member]
+                    member_tiles = slice(member * GROUP_TILES, (member + 1) * GROUP_TILES)
+                    nc.gpsimd.tensor_tensor(
+                        out=scaled[:],
+                        in0=scaled[:],
+                        in1=alpha[:, member_tiles].unsqueeze(2).to_broadcast([P, GROUP_TILES, CLASSES]),
+                        op=ALU.mult,
+                    )
 
-        cond, alpha = gate_weights(nc, gate, sums)
 
         for g in range(GROUPS):
             tiles = slice(g * GROUP_TILES, (g + 1) * GROUP_TILES)
             e_f = keep.tile([P, GROUP_TILES, CLASSES], F32, name="e_f_%d" % g)
             sum_f = small.tile([P, GROUP_TILES], F32, name="sum_f")
-            softmax_numerators(net_f, x_quantised[g], e_f, sum_f[:])
+            softmax_numerators(net_f, x_quantised[g], e_f, sum_f[:], 0)
+            member = g % HALF_GROUPS
             beta = small.tile([P, GROUP_TILES], F32, name="beta")
             nc.vector.reciprocal(out=beta[:], in_=sum_f[:])
-            nc.vector.tensor_mul(out=beta[:], in0=beta[:], in1=cond[:, tiles])
+            nc.vector.tensor_mul(
+                out=beta[:],
+                in0=beta[:],
+                in1=cond[g // HALF_GROUPS][:, member * GROUP_TILES : (member + 1) * GROUP_TILES],
+            )
             for j in range(GROUP_TILES):
-                tile_index = g * GROUP_TILES + j
-                nc.scalar.activation(
-                    out=e_o[g][:, j, :],
-                    in_=e_o[g][:, j, :],
-                    func=ACT.Copy,
-                    scale=alpha[:, tile_index : tile_index + 1],
-                )
                 nc.vector.scalar_tensor_tensor(
                     out=e_f[:, j, :],
                     in0=e_f[:, j, :],

@@ -19,6 +19,7 @@ TILES = ROWS // P
 GROUP_TILES = 4
 GROUP_ROWS = GROUP_TILES * P
 GROUPS = TILES // GROUP_TILES
+STEPS = 2 * GROUPS
 HALF_GROUPS = GROUPS // 2
 HALF_TILES = TILES // 2
 WORDS = D_IN // 2
@@ -44,45 +45,53 @@ def mx_pass(nc, acc, stationary, moving):
     )
 
 
-def load_network(nc, keep, setup, net, w1, b1, w2, b2):
-    w1_raw = setup.tile([P, PACK, D_H], BF16, name="w1_raw_" + net)
-    nc.sync.dma_start(
+def copy_on(engine, out, in_):
+    engine.tensor_scalar(out=out, in0=in_, scalar1=1.0, scalar2=0.0, op0=ALU.mult, op1=ALU.add)
+
+
+def stage_network(nc, keep, net, engine, w1, b1, w2, b2):
+    w1_raw = keep.tile([P, PACK, D_H], BF16, name="w1_raw_" + net)
+    nc.scalar.dma_start(
         out=w1_raw[:].rearrange("p (u e) h -> p u e h", u=2),
         in_=w1.rearrange("(u p e) h -> p u e h", u=2, e=2),
     )
-    w1_grouped = setup.tile([P, D_H, PACK], BF16, name="w1_grouped_" + net, align_bytes=64)
-    nc.vector.tensor_copy(
-        out=w1_grouped[:].rearrange("p (t m) j -> p t m j", t=PACK),
-        in_=w1_raw[:].rearrange("p j (m t) -> p t m j", t=PACK),
+    w1_grouped = keep.tile([P, D_H, PACK], BF16, name="w1_grouped_" + net, align_bytes=64)
+    copy_on(
+        engine,
+        w1_grouped[:].rearrange("p (t m) j -> p t m j", t=PACK),
+        w1_raw[:].rearrange("p j (m t) -> p t m j", t=PACK),
     )
-    w1_codes = keep.tile([P, D_H], U32, name="w1_codes_" + net, align_bytes=64)
-    w1_scales = keep.tile([P, D_H], U8, name="w1_scales_" + net, align_bytes=64)
-    quantise(nc, w1_grouped[:].rearrange("p c j -> p (c j)"), w1_codes[:], w1_scales[:])
-
-    b1_raw = setup.tile([P, PACK], BF16, name="b1_raw_" + net)
+    b1_raw = keep.tile([P, PACK], BF16, name="b1_raw_" + net)
     nc.scalar.dma_start(out=b1_raw[:], in_=b1.rearrange("(p t) -> p t", t=PACK))
     b1_cols = keep.tile([P, PACK], F32, name="b1_cols_" + net)
-    nc.vector.tensor_copy(out=b1_cols[:], in_=b1_raw[:])
-
-    w2_raw = setup.tile([P, PACK, CLASSES], BF16, name="w2_raw_" + net)
+    copy_on(engine, b1_cols[:], b1_raw[:])
+    w2_raw = keep.tile([P, PACK, CLASSES], BF16, name="w2_raw_" + net)
     nc.scalar.dma_start(out=w2_raw[:], in_=w2.rearrange("(p t) c -> p t c", t=PACK))
-    w2_grouped = setup.tile([P, CLASSES, PACK], BF16, name="w2_grouped_" + net, align_bytes=64)
-    nc.vector.tensor_copy(out=w2_grouped[:], in_=w2_raw[:].rearrange("p t c -> p c t"))
-    w2_codes = keep.tile([P, CLASSES], U32, name="w2_codes_" + net, align_bytes=64)
-    w2_scales = keep.tile([P, CLASSES], U8, name="w2_scales_" + net, align_bytes=64)
-    quantise(nc, w2_grouped[:].rearrange("p c t -> p (c t)"), w2_codes[:], w2_scales[:])
-
-    b2_raw = setup.tile([P, CLASSES], BF16, name="b2_raw_" + net)
+    w2_grouped = keep.tile([P, CLASSES, PACK], BF16, name="w2_grouped_" + net, align_bytes=64)
+    copy_on(engine, w2_grouped[:], w2_raw[:].rearrange("p t c -> p c t"))
+    b2_raw = keep.tile([P, CLASSES], BF16, name="b2_raw_" + net)
     nc.scalar.dma_start(out=b2_raw[:], in_=b2.partition_broadcast(P))
     b2_rows = keep.tile([P, CLASSES], F32, name="b2_rows_" + net)
-    nc.vector.tensor_copy(out=b2_rows[:], in_=b2_raw[:])
-
+    copy_on(engine, b2_rows[:], b2_raw[:])
     return {
-        "w1": (w1_codes, w1_scales),
+        "w1_grouped": w1_grouped,
+        "w2_grouped": w2_grouped,
+        "w1": (
+            keep.tile([P, D_H], U32, name="w1_codes_" + net, align_bytes=64),
+            keep.tile([P, D_H], U8, name="w1_scales_" + net, align_bytes=64),
+        ),
+        "w2": (
+            keep.tile([P, CLASSES], U32, name="w2_codes_" + net, align_bytes=64),
+            keep.tile([P, CLASSES], U8, name="w2_scales_" + net, align_bytes=64),
+        ),
         "b1": b1_cols,
-        "w2": (w2_codes, w2_scales),
         "b2": b2_rows,
     }
+
+
+def quantise_network(nc, net):
+    quantise(nc, net["w1_grouped"][:].rearrange("p c j -> p (c j)"), net["w1"][0][:], net["w1"][1][:])
+    quantise(nc, net["w2_grouped"][:].rearrange("p c t -> p (c t)"), net["w2"][0][:], net["w2"][1][:])
 
 
 def gp_affine(nc, out, in_, mul, add):
@@ -154,157 +163,218 @@ def tile_combnethe_pa_t_kernel(tc, x, W1o, b1o, W2o, b2o, W1f, b1f, W2f, b2f, ou
     out_rows = out.rearrange("(p j) c -> p j c", j=TILES)
 
     with ExitStack() as pools:
+        pools.enter_context(tc.manual_schedule())
         keep = pools.enter_context(tc.tile_pool(name="keep", bufs=1))
-        x_pool = pools.enter_context(tc.tile_pool(name="x_pool", bufs=3))
-
-        def load_x(g):
-            x_sb = x_pool.tile([P, GROUP_TILES * D_IN], BF16, name="x_sb")
-            nc.sync.dma_start(
-                out=x_sb[:].rearrange("p (j k) -> p j k", j=GROUP_TILES),
-                in_=x_rows[:, g * GROUP_TILES : (g + 1) * GROUP_TILES, :],
-            )
-            return x_sb
-
-        x_next = load_x(0)
-
-        identity = keep.tile([P, P], F32, name="identity")
-        make_identity(nc, identity[:])
-        with tc.tile_pool(name="setup", bufs=1) as setup:
-            net_o = load_network(nc, keep, setup, "o", W1o, b1o, W2o, b2o)
-            net_f = load_network(nc, keep, setup, "f", W1f, b1f, W2f, b2f)
-
-        work = pools.enter_context(tc.tile_pool(name="work", bufs=3))
-        small = pools.enter_context(tc.tile_pool(name="small", bufs=4))
         gate = pools.enter_context(tc.tile_pool(name="gate", bufs=1))
+        two = pools.enter_context(tc.tile_pool(name="two", bufs=2))
+        three = pools.enter_context(tc.tile_pool(name="three", bufs=3))
         psum_x = pools.enter_context(tc.psum_pool(name="psum_x", bufs=2))
         psum_z = pools.enter_context(tc.psum_pool(name="psum_z", bufs=4))
         psum_l = pools.enter_context(tc.psum_pool(name="psum_l", bufs=2))
 
-        def quantise_x(g, x_sb):
-            x_words = x_sb[:].bitcast(F32)
-            x_grouped = work.tile([P, GROUP_ROWS * PACK], BF16, name="x_grouped", align_bytes=64)
-            grouped_words = x_grouped[:].bitcast(F32)
-            for half in range(2):
-                x_t = psum_x.tile([P, 2, 2, P], F32, name="x_t")
-                for jj in range(2):
-                    for u in range(2):
-                        first = (2 * half + jj) * WORDS + u * P
-                        nc.tensor.transpose(x_t[:, jj, u, :], x_words[:, first : first + P], identity[:])
-                nc.vector.tensor_copy(
-                    out=grouped_words[:, half * 2 * WORDS : (half + 1) * 2 * WORDS].rearrange(
-                        "p (j r u) -> p j r u", j=2, u=2
-                    ),
-                    in_=x_t[:].rearrange("p j u r -> p j r u"),
-                )
-            codes = keep.tile([P, GROUP_ROWS], U32, name="x_codes_%d" % g, align_bytes=64)
-            scales = keep.tile([P, GROUP_ROWS], U8, name="x_scales_%d" % g, align_bytes=64)
-            quantise(nc, x_grouped[:], codes[:], scales[:])
-            return codes, scales
-
-        def softmax_numerators(net, x_q, e, e_sum, vector_planes):
-            w1_codes, w1_scales = net["w1"]
-            planes = work.tile([P, PACK, GROUP_ROWS], BF16, name="planes")
-            for t in range(PACK):
-                z = psum_z.tile([P, GROUP_ROWS], F32, name="z")
-                cols = slice(t * P, (t + 1) * P)
-                mx_pass(nc, z[:], (w1_codes[:, cols], w1_scales[:, cols]), (x_q[0][:], x_q[1][:]))
-                bias = net["b1"][:, t : t + 1]
-                if t < PACK - vector_planes:
-                    nc.scalar.activation(out=planes[:, t, :], in_=z[:], func=ACT.Relu, bias=bias, scale=1.0)
-                else:
-                    nc.vector.tensor_scalar(
-                        out=planes[:, t, :], in0=z[:], scalar1=bias, scalar2=0.0, op0=ALU.add, op1=ALU.max
-                    )
-            h_grouped = work.tile([P, GROUP_ROWS, PACK], BF16, name="h_grouped", align_bytes=64)
-            nc.vector.tensor_copy(
-                out=h_grouped[:].rearrange("p (c i) t -> p c t i", i=4),
-                in_=planes[:].rearrange("p t (c i) -> p c t i", i=4),
-            )
-            h_codes = work.tile([P, GROUP_ROWS], U32, name="h_codes", align_bytes=64)
-            h_scales = work.tile([P, GROUP_ROWS], U8, name="h_scales", align_bytes=64)
-            quantise(nc, h_grouped[:].rearrange("p r t -> p (r t)"), h_codes[:], h_scales[:])
-
-            acc = psum_l.tile([P, GROUP_TILES, CLASSES], F32, name="acc")
-            for j in range(GROUP_TILES):
-                cols = slice(j * P, (j + 1) * P)
-                mx_pass(nc, acc[:, j, :], (h_codes[:, cols], h_scales[:, cols]), (net["w2"][0][:], net["w2"][1][:]))
-            logits = work.tile([P, GROUP_TILES, CLASSES], F32, name="logits")
-            nc.vector.tensor_tensor(
-                out=logits[:],
-                in0=acc[:],
-                in1=net["b2"][:].unsqueeze(1).to_broadcast([P, GROUP_TILES, CLASSES]),
-                op=ALU.add,
-            )
-            neg_max = small.tile([P, GROUP_TILES], F32, name="neg_max")
-            nc.vector.tensor_reduce(out=neg_max[:], in_=logits[:], axis=AXIS.X, op=ALU.max, negate=True)
-            for j in range(GROUP_TILES):
-                nc.scalar.activation(
-                    out=e[:, j, :],
-                    in_=logits[:, j, :],
-                    func=ACT.Exp,
-                    bias=neg_max[:, j : j + 1],
-                    scale=1.0,
-                    accum_out=e_sum[:, j : j + 1],
-                )
+        identity = keep.tile([P, P], F32, name="identity")
+        make_identity(nc, identity[:])
+        nets = [
+            stage_network(nc, keep, "o", nc.vector, W1o, b1o, W2o, b2o),
+            stage_network(nc, keep, "f", nc.gpsimd, W1f, b1f, W2f, b2f),
+        ]
+        quantise_network(nc, nets[0])
 
         sums = {}
         for power in ("e1", "e2", "e4", "e8"):
             sums[power] = gate.tile([P, TILES], F32, name="sum_" + power)
-        x_quantised = []
-        e_o = []
         cond = []
-        for g in range(GROUPS):
-            x_sb = x_next
-            if g + 1 < GROUPS:
-                x_next = load_x(g + 1)
-            x_quantised.append(quantise_x(g, x_sb))
-            tiles = slice(g * GROUP_TILES, (g + 1) * GROUP_TILES)
-            e_o.append(keep.tile([P, GROUP_TILES, CLASSES], F32, name="e_o_%d" % g))
-            softmax_numerators(net_o, x_quantised[g], e_o[g], sums["e1"][:, tiles], g % 2)
-            powers = work.tile([P, GROUP_TILES, CLASSES], F32, name="powers")
+        x_sb, x_t, x_grouped, x_q = {}, {}, {}, {}
+        planes, z_left, h_grouped, h_q, acc, logits, neg_max, e, e_sum, beta = {}, {}, {}, {}, {}, {}, {}, {}, {}, {}
+
+        def load_x(g):
+            x_sb[g] = three.tile([P, GROUP_TILES * D_IN], BF16, name="x_sb")
+            nc.sync.dma_start(
+                out=x_sb[g][:].rearrange("p (j k) -> p j k", j=GROUP_TILES),
+                in_=x_rows[:, g * GROUP_TILES : (g + 1) * GROUP_TILES, :],
+            )
+
+        def transpose_x(g):
+            x_words = x_sb[g][:].bitcast(F32)
+            x_t[g] = []
+            for half in range(2):
+                bank = psum_x.tile([P, 2, 2, P], F32, name="x_t")
+                for jj in range(2):
+                    for u in range(2):
+                        first = (2 * half + jj) * WORDS + u * P
+                        nc.tensor.transpose(bank[:, jj, u, :], x_words[:, first : first + P], identity[:])
+                x_t[g].append(bank)
+
+        def copy_x_out(g, half):
+            if half == 0:
+                x_grouped[g] = two.tile([P, GROUP_ROWS * PACK], BF16, name="x_grouped", align_bytes=64)
+            grouped_words = x_grouped[g][:].bitcast(F32)
+            nc.vector.tensor_copy(
+                out=grouped_words[:, half * 2 * WORDS : (half + 1) * 2 * WORDS].rearrange(
+                    "p (j r u) -> p j r u", j=2, u=2
+                ),
+                in_=x_t[g][half][:].rearrange("p j u r -> p j r u"),
+            )
+
+        def quantise_x(g):
+            x_q[g] = (
+                keep.tile([P, GROUP_ROWS], U32, name="x_codes_%d" % g, align_bytes=64),
+                keep.tile([P, GROUP_ROWS], U8, name="x_scales_%d" % g, align_bytes=64),
+            )
+            quantise(nc, x_grouped[g][:], x_q[g][0][:], x_q[g][1][:])
+
+        def hidden_layer(s):
+            net = nets[s // GROUPS]
+            codes, scales = net["w1"]
+            rows = x_q[s % GROUPS]
+            planes[s] = two.tile([P, PACK, GROUP_ROWS], BF16, name="planes")
+            for t in range(PACK):
+                z = psum_z.tile([P, GROUP_ROWS], F32, name="z")
+                cols = slice(t * P, (t + 1) * P)
+                mx_pass(nc, z[:], (codes[:, cols], scales[:, cols]), (rows[0][:], rows[1][:]))
+                if t == PACK - 1 and s < GROUPS and s % 2 == 1:
+                    z_left[s] = z
+                else:
+                    nc.scalar.activation(
+                        out=planes[s][:, t, :], in_=z[:], func=ACT.Relu, bias=net["b1"][:, t : t + 1], scale=1.0
+                    )
+
+        def vector_relu(s):
+            if s in z_left:
+                t = PACK - 1
+                nc.vector.tensor_scalar(
+                    out=planes[s][:, t, :],
+                    in0=z_left[s][:],
+                    scalar1=nets[s // GROUPS]["b1"][:, t : t + 1],
+                    scalar2=0.0,
+                    op0=ALU.add,
+                    op1=ALU.max,
+                )
+
+        def regroup_h(s):
+            h_grouped[s] = two.tile([P, GROUP_ROWS, PACK], BF16, name="h_grouped", align_bytes=64)
+            nc.vector.tensor_copy(
+                out=h_grouped[s][:].rearrange("p (c i) t -> p c t i", i=4),
+                in_=planes[s][:].rearrange("p t (c i) -> p c t i", i=4),
+            )
+
+        def quantise_h(s):
+            h_q[s] = (
+                two.tile([P, GROUP_ROWS], U32, name="h_codes", align_bytes=64),
+                two.tile([P, GROUP_ROWS], U8, name="h_scales", align_bytes=64),
+            )
+            quantise(nc, h_grouped[s][:].rearrange("p r t -> p (r t)"), h_q[s][0][:], h_q[s][1][:])
+
+        def head(s):
+            w2 = nets[s // GROUPS]["w2"]
+            acc[s] = psum_l.tile([P, GROUP_TILES, CLASSES], F32, name="acc")
+            for j in range(GROUP_TILES):
+                cols = slice(j * P, (j + 1) * P)
+                mx_pass(nc, acc[s][:, j, :], (h_q[s][0][:, cols], h_q[s][1][:, cols]), (w2[0][:], w2[1][:]))
+
+        def add_bias(s):
+            logits[s] = three.tile([P, GROUP_TILES, CLASSES], F32, name="logits")
+            nc.vector.tensor_tensor(
+                out=logits[s][:],
+                in0=acc[s][:],
+                in1=nets[s // GROUPS]["b2"][:].unsqueeze(1).to_broadcast([P, GROUP_TILES, CLASSES]),
+                op=ALU.add,
+            )
+
+        def row_max(s):
+            neg_max[s] = three.tile([P, GROUP_TILES], F32, name="neg_max")
+            nc.vector.tensor_reduce(out=neg_max[s][:], in_=logits[s][:], axis=AXIS.X, op=ALU.max, negate=True)
+
+        def exponentials(s):
+            if s < GROUPS:
+                e[s] = keep.tile([P, GROUP_TILES, CLASSES], F32, name="e_o_%d" % s)
+                e_sum[s] = sums["e1"][:, s * GROUP_TILES : (s + 1) * GROUP_TILES]
+            else:
+                e[s] = three.tile([P, GROUP_TILES, CLASSES], F32, name="e_f")
+                e_sum[s] = three.tile([P, GROUP_TILES], F32, name="sum_f")
+            for j in range(GROUP_TILES):
+                nc.scalar.activation(
+                    out=e[s][:, j, :],
+                    in_=logits[s][:, j, :],
+                    func=ACT.Exp,
+                    bias=neg_max[s][:, j : j + 1],
+                    scale=1.0,
+                    accum_out=e_sum[s][:, j : j + 1],
+                )
+
+        def power_sums(s):
+            powers = two.tile([P, GROUP_TILES, CLASSES], F32, name="powers")
             for power in ("e2", "e4", "e8"):
                 for j in range(GROUP_TILES):
                     nc.scalar.activation(
                         out=powers[:, j, :],
-                        in_=e_o[g][:, j, :] if power == "e2" else powers[:, j, :],
+                        in_=e[s][:, j, :] if power == "e2" else powers[:, j, :],
                         func=ACT.Square,
-                        accum_out=sums[power][:, g * GROUP_TILES + j : g * GROUP_TILES + j + 1],
-                    )
-            if (g + 1) % HALF_GROUPS == 0:
-                half = g // HALF_GROUPS
-                cond_half, alpha = gate_weights(nc, gate, sums, half)
-                cond.append(cond_half)
-                for member in range(HALF_GROUPS):
-                    scaled = e_o[half * HALF_GROUPS + member]
-                    member_tiles = slice(member * GROUP_TILES, (member + 1) * GROUP_TILES)
-                    nc.gpsimd.tensor_tensor(
-                        out=scaled[:],
-                        in0=scaled[:],
-                        in1=alpha[:, member_tiles].unsqueeze(2).to_broadcast([P, GROUP_TILES, CLASSES]),
-                        op=ALU.mult,
+                        accum_out=sums[power][:, s * GROUP_TILES + j : s * GROUP_TILES + j + 1],
                     )
 
+        def gate_half(half):
+            cond_half, alpha = gate_weights(nc, gate, sums, half)
+            cond.append(cond_half)
+            for member in range(HALF_GROUPS):
+                scaled = e[half * HALF_GROUPS + member]
+                member_tiles = slice(member * GROUP_TILES, (member + 1) * GROUP_TILES)
+                nc.gpsimd.tensor_tensor(
+                    out=scaled[:],
+                    in0=scaled[:],
+                    in1=alpha[:, member_tiles].unsqueeze(2).to_broadcast([P, GROUP_TILES, CLASSES]),
+                    op=ALU.mult,
+                )
 
-        for g in range(GROUPS):
-            tiles = slice(g * GROUP_TILES, (g + 1) * GROUP_TILES)
-            e_f = keep.tile([P, GROUP_TILES, CLASSES], F32, name="e_f_%d" % g)
-            sum_f = small.tile([P, GROUP_TILES], F32, name="sum_f")
-            softmax_numerators(net_f, x_quantised[g], e_f, sum_f[:], 0)
+        def blend_reciprocal(s):
+            beta[s] = three.tile([P, GROUP_TILES], F32, name="beta")
+            nc.vector.reciprocal(out=beta[s][:], in_=e_sum[s][:])
+
+        def blend_beta(s):
+            g = s - GROUPS
             member = g % HALF_GROUPS
-            beta = small.tile([P, GROUP_TILES], F32, name="beta")
-            nc.vector.reciprocal(out=beta[:], in_=sum_f[:])
             nc.vector.tensor_mul(
-                out=beta[:],
-                in0=beta[:],
+                out=beta[s][:],
+                in0=beta[s][:],
                 in1=cond[g // HALF_GROUPS][:, member * GROUP_TILES : (member + 1) * GROUP_TILES],
             )
+
+        def blend_and_store(s):
+            g = s - GROUPS
             for j in range(GROUP_TILES):
                 nc.vector.scalar_tensor_tensor(
-                    out=e_f[:, j, :],
-                    in0=e_f[:, j, :],
-                    scalar=beta[:, j : j + 1],
-                    in1=e_o[g][:, j, :],
+                    out=e[s][:, j, :],
+                    in0=e[s][:, j, :],
+                    scalar=beta[s][:, j : j + 1],
+                    in1=e[g][:, j, :],
                     op0=ALU.mult,
                     op1=ALU.add,
                 )
-            nc.sync.dma_start(out=out_rows[:, tiles, :], in_=e_f[:])
+            nc.sync.dma_start(out=out_rows[:, g * GROUP_TILES : (g + 1) * GROUP_TILES, :], in_=e[s][:])
+
+        def run(stage, index, first, last):
+            if first <= index < last:
+                stage(index)
+
+        for i in range(-4, STEPS + 4):
+            run(load_x, i + 4, 0, GROUPS)
+            run(hidden_layer, i + 1, 0, STEPS)
+            run(regroup_h, i, 0, STEPS)
+            run(lambda g: copy_x_out(g, 0), i + 2, 0, GROUPS)
+            run(blend_reciprocal, i - 3, GROUPS, STEPS)
+            run(quantise_h, i, 0, STEPS)
+            run(lambda g: copy_x_out(g, 1), i + 2, 0, GROUPS)
+            run(vector_relu, i + 1, 0, GROUPS)
+            run(transpose_x, i + 3, 0, GROUPS)
+            run(head, i, 0, STEPS)
+            run(add_bias, i - 1, 0, STEPS)
+            run(quantise_x, i + 2, 0, GROUPS)
+            run(blend_beta, i - 3, GROUPS, STEPS)
+            run(row_max, i - 1, 0, STEPS)
+            run(exponentials, i - 2, 0, STEPS)
+            run(power_sums, i - 2, 0, GROUPS)
+            run(blend_and_store, i - 3, GROUPS, STEPS)
+            if i == 0:
+                quantise_network(nc, nets[1])
+            if i - 3 in (HALF_GROUPS - 1, GROUPS - 1):
+                gate_half((i - 3) // HALF_GROUPS)

@@ -183,7 +183,7 @@ def tile_combnethe_pa_t_kernel(tc, x, W1o, b1o, W2o, b2o, W1f, b1f, W2f, b2f, ou
         sums = {}
         for power in ("e1", "e2", "e4", "e8"):
             sums[power] = gate.tile([P, TILES], F32, name="sum_" + power)
-        cond = []
+        cond, alpha = [], []
         x_sb, x_t, x_grouped, x_q = {}, {}, {}, {}
         planes, z_left, h_grouped, h_q, acc, logits, neg_max, e, e_sum, beta = {}, {}, {}, {}, {}, {}, {}, {}, {}, {}
 
@@ -314,16 +314,19 @@ def tile_combnethe_pa_t_kernel(tc, x, W1o, b1o, W2o, b2o, W1f, b1f, W2f, b2f, ou
                     )
 
         def gate_half(half):
-            cond_half, alpha = gate_weights(nc, gate, sums, half)
+            cond_half, alpha_half = gate_weights(nc, gate, sums, half)
             cond.append(cond_half)
-            for member in range(HALF_GROUPS):
-                scaled = e[half * HALF_GROUPS + member]
-                member_tiles = slice(member * GROUP_TILES, (member + 1) * GROUP_TILES)
-                nc.gpsimd.tensor_tensor(
-                    out=scaled[:],
-                    in0=scaled[:],
-                    in1=alpha[:, member_tiles].unsqueeze(2).to_broadcast([P, GROUP_TILES, CLASSES]),
-                    op=ALU.mult,
+            alpha.append(alpha_half)
+
+        def blend_scale_o(s):
+            g = s - GROUPS
+            for j in range(GROUP_TILES):
+                column = (g % HALF_GROUPS) * GROUP_TILES + j
+                nc.scalar.activation(
+                    out=e[g][:, j, :],
+                    in_=e[g][:, j, :],
+                    func=ACT.Copy,
+                    scale=alpha[g // HALF_GROUPS][:, column : column + 1],
                 )
 
         def blend_reciprocal(s):
@@ -373,6 +376,7 @@ def tile_combnethe_pa_t_kernel(tc, x, W1o, b1o, W2o, b2o, W1f, b1f, W2f, b2f, ou
             run(row_max, i - 1, 0, STEPS)
             run(exponentials, i - 2, 0, STEPS)
             run(power_sums, i - 2, 0, GROUPS)
+            run(blend_scale_o, i - 2, GROUPS, STEPS)
             run(blend_and_store, i - 3, GROUPS, STEPS)
             if i == 0:
                 quantise_network(nc, nets[1])

@@ -20,8 +20,7 @@ GROUP_TILES = 4
 GROUP_ROWS = GROUP_TILES * P
 GROUPS = TILES // GROUP_TILES
 STEPS = 2 * GROUPS
-HALF_GROUPS = GROUPS // 2
-HALF_TILES = TILES // 2
+BLEND_LAG = 6
 WORDS = D_IN // 2
 TAU = 0.5
 SERIES_STEPS = 3
@@ -49,7 +48,7 @@ def copy_on(engine, out, in_):
     engine.tensor_scalar(out=out, in0=in_, scalar1=1.0, scalar2=0.0, op0=ALU.mult, op1=ALU.add)
 
 
-def stage_network(nc, keep, net, engine, w1, b1, w2, b2):
+def stage_network(nc, keep, net, w1_engine, w1, b1, w2, b2):
     w1_raw = keep.tile([P, PACK, D_H], BF16, name="w1_raw_" + net)
     nc.scalar.dma_start(
         out=w1_raw[:].rearrange("p (u e) h -> p u e h", u=2),
@@ -57,22 +56,22 @@ def stage_network(nc, keep, net, engine, w1, b1, w2, b2):
     )
     w1_grouped = keep.tile([P, D_H, PACK], BF16, name="w1_grouped_" + net, align_bytes=64)
     copy_on(
-        engine,
+        w1_engine,
         w1_grouped[:].rearrange("p (t m) j -> p t m j", t=PACK),
         w1_raw[:].rearrange("p j (m t) -> p t m j", t=PACK),
     )
     b1_raw = keep.tile([P, PACK], BF16, name="b1_raw_" + net)
     nc.scalar.dma_start(out=b1_raw[:], in_=b1.rearrange("(p t) -> p t", t=PACK))
     b1_cols = keep.tile([P, PACK], F32, name="b1_cols_" + net)
-    copy_on(engine, b1_cols[:], b1_raw[:])
+    copy_on(nc.gpsimd, b1_cols[:], b1_raw[:])
     w2_raw = keep.tile([P, PACK, CLASSES], BF16, name="w2_raw_" + net)
     nc.scalar.dma_start(out=w2_raw[:], in_=w2.rearrange("(p t) c -> p t c", t=PACK))
     w2_grouped = keep.tile([P, CLASSES, PACK], BF16, name="w2_grouped_" + net, align_bytes=64)
-    copy_on(engine, w2_grouped[:], w2_raw[:].rearrange("p t c -> p c t"))
+    copy_on(nc.gpsimd, w2_grouped[:], w2_raw[:].rearrange("p t c -> p c t"))
     b2_raw = keep.tile([P, CLASSES], BF16, name="b2_raw_" + net)
     nc.scalar.dma_start(out=b2_raw[:], in_=b2.partition_broadcast(P))
     b2_rows = keep.tile([P, CLASSES], F32, name="b2_rows_" + net)
-    copy_on(engine, b2_rows[:], b2_raw[:])
+    copy_on(nc.gpsimd, b2_rows[:], b2_raw[:])
     return {
         "w1_grouped": w1_grouped,
         "w2_grouped": w2_grouped,
@@ -103,9 +102,9 @@ def gp_mul(nc, out, in0, in1):
 
 
 def inverse_series(nc, gate, total, m, name):
-    b = gate.tile([P, HALF_TILES], F32, name="b_" + name)
-    a = gate.tile([P, HALF_TILES], F32, name="a_" + name)
-    one_plus_b = gate.tile([P, HALF_TILES], F32, name="one_plus_b_" + name)
+    b = gate.tile([P, TILES], F32, name="b_" + name)
+    a = gate.tile([P, TILES], F32, name="a_" + name)
+    one_plus_b = gate.tile([P, TILES], F32, name="one_plus_b_" + name)
     gp_affine(nc, b[:], total, -2.0 / m, 1.0)
     gp_affine(nc, a[:], b[:], 1.0, 1.0)
     for step in range(SERIES_STEPS):
@@ -115,40 +114,37 @@ def inverse_series(nc, gate, total, m, name):
     return a
 
 
-def gate_weights(nc, gate, sums, half):
-    cols = slice(half * HALF_TILES, (half + 1) * HALF_TILES)
-    tag = "_%d" % half
-
+def gate_weights(nc, gate, sums):
     def new(name):
-        return gate.tile([P, HALF_TILES], F32, name=name + tag)
+        return gate.tile([P, TILES], F32, name=name)
 
     recip1, recip2, recip4, recip8 = new("recip1"), new("recip2"), new("recip4"), new("recip8")
-    nc.vector.reciprocal(out=recip1[:], in_=sums["e1"][:, cols])
+    nc.vector.reciprocal(out=recip1[:], in_=sums["e1"][:])
     gp_mul(nc, recip2[:], recip1[:], recip1[:])
     gp_mul(nc, recip4[:], recip2[:], recip2[:])
     gp_mul(nc, recip8[:], recip4[:], recip4[:])
 
     total0, inv0, scale1 = new("total0"), new("inv0"), new("scale1")
-    gp_mul(nc, total0[:], sums["e2"][:, cols], recip2[:])
+    gp_mul(nc, total0[:], sums["e2"][:], recip2[:])
     gp_affine(nc, total0[:], total0[:], 1.0, TAU**2)
     m0 = 2.0 + TAU**2
-    a0 = inverse_series(nc, gate, total0[:], m0, "0" + tag)
+    a0 = inverse_series(nc, gate, total0[:], m0, "0")
     gp_affine(nc, inv0[:], a0[:], 2.0 / m0, 0.0)
     gp_mul(nc, scale1[:], inv0[:], inv0[:])
 
     total1, scale2 = new("total1"), new("scale2")
-    gp_mul(nc, total1[:], sums["e4"][:, cols], recip4[:])
+    gp_mul(nc, total1[:], sums["e4"][:], recip4[:])
     gp_affine(nc, total1[:], total1[:], 1.0, TAU**4)
     gp_mul(nc, total1[:], total1[:], scale1[:])
-    a1 = inverse_series(nc, gate, total1[:], 2.0, "1" + tag)
+    a1 = inverse_series(nc, gate, total1[:], 2.0, "1")
     gp_mul(nc, scale2[:], scale1[:], a1[:])
     gp_mul(nc, scale2[:], scale2[:], scale2[:])
 
     total2, cond, alpha = new("total2"), new("cond"), new("alpha")
-    gp_mul(nc, total2[:], sums["e8"][:, cols], recip8[:])
+    gp_mul(nc, total2[:], sums["e8"][:], recip8[:])
     gp_affine(nc, total2[:], total2[:], 1.0, TAU**8)
     gp_mul(nc, total2[:], total2[:], scale2[:])
-    a2 = inverse_series(nc, gate, total2[:], 2.0, "2" + tag)
+    a2 = inverse_series(nc, gate, total2[:], 2.0, "2")
     gp_mul(nc, cond[:], scale2[:], a2[:])
     gp_affine(nc, cond[:], cond[:], TAU**8, 0.0)
 
@@ -168,6 +164,7 @@ def tile_combnethe_pa_t_kernel(tc, x, W1o, b1o, W2o, b2o, W1f, b1f, W2f, b2f, ou
         gate = pools.enter_context(tc.tile_pool(name="gate", bufs=1))
         two = pools.enter_context(tc.tile_pool(name="two", bufs=2))
         three = pools.enter_context(tc.tile_pool(name="three", bufs=3))
+        lagged = pools.enter_context(tc.tile_pool(name="lagged", bufs=3 + BLEND_LAG))
         psum_x = pools.enter_context(tc.psum_pool(name="psum_x", bufs=2))
         psum_z = pools.enter_context(tc.psum_pool(name="psum_z", bufs=4))
         psum_l = pools.enter_context(tc.psum_pool(name="psum_l", bufs=2))
@@ -183,8 +180,8 @@ def tile_combnethe_pa_t_kernel(tc, x, W1o, b1o, W2o, b2o, W1f, b1f, W2f, b2f, ou
         sums = {}
         for power in ("e1", "e2", "e4", "e8"):
             sums[power] = gate.tile([P, TILES], F32, name="sum_" + power)
-        cond, alpha = [], []
         x_sb, x_t, x_grouped, x_q = {}, {}, {}, {}
+        gate_out = {}
         planes, z_left, h_grouped, h_q, acc, logits, neg_max, e, e_sum, beta = {}, {}, {}, {}, {}, {}, {}, {}, {}, {}
 
         def load_x(g):
@@ -290,8 +287,8 @@ def tile_combnethe_pa_t_kernel(tc, x, W1o, b1o, W2o, b2o, W1f, b1f, W2f, b2f, ou
                 e[s] = keep.tile([P, GROUP_TILES, CLASSES], F32, name="e_o_%d" % s)
                 e_sum[s] = sums["e1"][:, s * GROUP_TILES : (s + 1) * GROUP_TILES]
             else:
-                e[s] = three.tile([P, GROUP_TILES, CLASSES], F32, name="e_f")
-                e_sum[s] = three.tile([P, GROUP_TILES], F32, name="sum_f")
+                e[s] = lagged.tile([P, GROUP_TILES, CLASSES], F32, name="e_f")
+                e_sum[s] = lagged.tile([P, GROUP_TILES], F32, name="sum_f")
             for j in range(GROUP_TILES):
                 nc.scalar.activation(
                     out=e[s][:, j, :],
@@ -313,20 +310,15 @@ def tile_combnethe_pa_t_kernel(tc, x, W1o, b1o, W2o, b2o, W1f, b1f, W2f, b2f, ou
                         accum_out=sums[power][:, s * GROUP_TILES + j : s * GROUP_TILES + j + 1],
                     )
 
-        def gate_half(half):
-            cond_half, alpha_half = gate_weights(nc, gate, sums, half)
-            cond.append(cond_half)
-            alpha.append(alpha_half)
-
         def blend_scale_o(s):
             g = s - GROUPS
             for j in range(GROUP_TILES):
-                column = (g % HALF_GROUPS) * GROUP_TILES + j
+                column = g * GROUP_TILES + j
                 nc.scalar.activation(
                     out=e[g][:, j, :],
                     in_=e[g][:, j, :],
                     func=ACT.Copy,
-                    scale=alpha[g // HALF_GROUPS][:, column : column + 1],
+                    scale=gate_out["alpha"][:, column : column + 1],
                 )
 
         def blend_reciprocal(s):
@@ -335,11 +327,10 @@ def tile_combnethe_pa_t_kernel(tc, x, W1o, b1o, W2o, b2o, W1f, b1f, W2f, b2f, ou
 
         def blend_beta(s):
             g = s - GROUPS
-            member = g % HALF_GROUPS
             nc.vector.tensor_mul(
                 out=beta[s][:],
                 in0=beta[s][:],
-                in1=cond[g // HALF_GROUPS][:, member * GROUP_TILES : (member + 1) * GROUP_TILES],
+                in1=gate_out["cond"][:, g * GROUP_TILES : (g + 1) * GROUP_TILES],
             )
 
         def blend_and_store(s):
@@ -359,12 +350,13 @@ def tile_combnethe_pa_t_kernel(tc, x, W1o, b1o, W2o, b2o, W1f, b1f, W2f, b2f, ou
             if first <= index < last:
                 stage(index)
 
-        for i in range(-4, STEPS + 4):
+        for i in range(-4, STEPS + BLEND_LAG + 4):
+            blended = i - 3 - BLEND_LAG
             run(load_x, i + 4, 0, GROUPS)
             run(hidden_layer, i + 1, 0, STEPS)
             run(regroup_h, i, 0, STEPS)
             run(lambda g: copy_x_out(g, 0), i + 2, 0, GROUPS)
-            run(blend_reciprocal, i - 3, GROUPS, STEPS)
+            run(blend_reciprocal, blended, GROUPS, STEPS)
             run(quantise_h, i, 0, STEPS)
             run(lambda g: copy_x_out(g, 1), i + 2, 0, GROUPS)
             run(vector_relu, i + 1, 0, GROUPS)
@@ -372,13 +364,13 @@ def tile_combnethe_pa_t_kernel(tc, x, W1o, b1o, W2o, b2o, W1f, b1f, W2f, b2f, ou
             run(head, i, 0, STEPS)
             run(add_bias, i - 1, 0, STEPS)
             run(quantise_x, i + 2, 0, GROUPS)
-            run(blend_beta, i - 3, GROUPS, STEPS)
+            run(blend_beta, blended, GROUPS, STEPS)
             run(row_max, i - 1, 0, STEPS)
             run(exponentials, i - 2, 0, STEPS)
             run(power_sums, i - 2, 0, GROUPS)
-            run(blend_scale_o, i - 2, GROUPS, STEPS)
-            run(blend_and_store, i - 3, GROUPS, STEPS)
+            run(blend_scale_o, blended + 1, GROUPS, STEPS)
+            run(blend_and_store, blended, GROUPS, STEPS)
             if i == 0:
                 quantise_network(nc, nets[1])
-            if i - 3 in (HALF_GROUPS - 1, GROUPS - 1):
-                gate_half((i - 3) // HALF_GROUPS)
+            if i - 3 == GROUPS - 1:
+                gate_out["cond"], gate_out["alpha"] = gate_weights(nc, gate, sums)

@@ -20,7 +20,8 @@ GROUP_TILES = 4
 GROUP_ROWS = GROUP_TILES * P
 GROUPS = TILES // GROUP_TILES
 STEPS = 2 * GROUPS
-BLEND_LAG = 6
+HALF_GROUPS = GROUPS // 2
+HALF_TILES = TILES // 2
 WORDS = D_IN // 2
 TAU = 0.5
 SERIES_STEPS = 3
@@ -44,48 +45,43 @@ def mx_pass(nc, acc, stationary, moving):
     )
 
 
-def copy_on(engine, out, in_):
-    engine.tensor_scalar(out=out, in0=in_, scalar1=1.0, scalar2=0.0, op0=ALU.mult, op1=ALU.add)
-
-
-def stage_network(nc, keep, net, w1_engine, w1, b1, w2, b2):
-    w1_raw = keep.tile([P, PACK, D_H], BF16, name="w1_raw_" + net)
-    nc.scalar.dma_start(
-        out=w1_raw[:].rearrange("p (u e) h -> p u e h", u=2),
-        in_=w1.rearrange("(u p e) h -> p u e h", u=2, e=2),
-    )
-    w1_grouped = keep.tile([P, D_H, PACK], BF16, name="w1_grouped_" + net, align_bytes=64)
-    copy_on(
-        w1_engine,
-        w1_grouped[:].rearrange("p (t m) j -> p t m j", t=PACK),
-        w1_raw[:].rearrange("p j (m t) -> p t m j", t=PACK),
-    )
-    b1_raw = keep.tile([P, PACK], BF16, name="b1_raw_" + net)
-    nc.scalar.dma_start(out=b1_raw[:], in_=b1.rearrange("(p t) -> p t", t=PACK))
-    b1_cols = keep.tile([P, PACK], F32, name="b1_cols_" + net)
-    copy_on(nc.gpsimd, b1_cols[:], b1_raw[:])
-    w2_raw = keep.tile([P, PACK, CLASSES], BF16, name="w2_raw_" + net)
-    nc.scalar.dma_start(out=w2_raw[:], in_=w2.rearrange("(p t) c -> p t c", t=PACK))
-    w2_grouped = keep.tile([P, CLASSES, PACK], BF16, name="w2_grouped_" + net, align_bytes=64)
-    copy_on(nc.gpsimd, w2_grouped[:], w2_raw[:].rearrange("p t c -> p c t"))
-    b2_raw = keep.tile([P, CLASSES], BF16, name="b2_raw_" + net)
-    nc.scalar.dma_start(out=b2_raw[:], in_=b2.partition_broadcast(P))
-    b2_rows = keep.tile([P, CLASSES], F32, name="b2_rows_" + net)
-    copy_on(nc.gpsimd, b2_rows[:], b2_raw[:])
-    return {
-        "w1_grouped": w1_grouped,
-        "w2_grouped": w2_grouped,
+def load_network(nc, keep, net, w1, b1, w2, b2):
+    tiles = {
+        "w1_raw": keep.tile([P, PACK, D_H], BF16, name="w1_raw_" + net),
+        "w1_grouped": keep.tile([P, D_H, PACK], BF16, name="w1_grouped_" + net, align_bytes=64),
         "w1": (
             keep.tile([P, D_H], U32, name="w1_codes_" + net, align_bytes=64),
             keep.tile([P, D_H], U8, name="w1_scales_" + net, align_bytes=64),
         ),
+        "b1_raw": keep.tile([P, PACK], BF16, name="b1_raw_" + net),
+        "b1": keep.tile([P, PACK], F32, name="b1_cols_" + net),
+        "w2_raw": keep.tile([P, PACK, CLASSES], BF16, name="w2_raw_" + net),
+        "w2_grouped": keep.tile([P, CLASSES, PACK], BF16, name="w2_grouped_" + net, align_bytes=64),
         "w2": (
             keep.tile([P, CLASSES], U32, name="w2_codes_" + net, align_bytes=64),
             keep.tile([P, CLASSES], U8, name="w2_scales_" + net, align_bytes=64),
         ),
-        "b1": b1_cols,
-        "b2": b2_rows,
+        "b2_raw": keep.tile([P, CLASSES], BF16, name="b2_raw_" + net),
+        "b2": keep.tile([P, CLASSES], F32, name="b2_rows_" + net),
     }
+    nc.scalar.dma_start(
+        out=tiles["w1_raw"][:].rearrange("p (u e) h -> p u e h", u=2),
+        in_=w1.rearrange("(u p e) h -> p u e h", u=2, e=2),
+    )
+    nc.scalar.dma_start(out=tiles["b1_raw"][:], in_=b1.rearrange("(p t) -> p t", t=PACK))
+    nc.scalar.dma_start(out=tiles["w2_raw"][:], in_=w2.rearrange("(p t) c -> p t c", t=PACK))
+    nc.scalar.dma_start(out=tiles["b2_raw"][:], in_=b2.partition_broadcast(P))
+    return tiles
+
+
+def lay_out_network(net, copy):
+    copy(
+        net["w1_grouped"][:].rearrange("p (t m) j -> p t m j", t=PACK),
+        net["w1_raw"][:].rearrange("p j (m t) -> p t m j", t=PACK),
+    )
+    copy(net["b1"][:], net["b1_raw"][:])
+    copy(net["w2_grouped"][:], net["w2_raw"][:].rearrange("p t c -> p c t"))
+    copy(net["b2"][:], net["b2_raw"][:])
 
 
 def quantise_network(nc, net):
@@ -102,9 +98,9 @@ def gp_mul(nc, out, in0, in1):
 
 
 def inverse_series(nc, gate, total, m, name):
-    b = gate.tile([P, TILES], F32, name="b_" + name)
-    a = gate.tile([P, TILES], F32, name="a_" + name)
-    one_plus_b = gate.tile([P, TILES], F32, name="one_plus_b_" + name)
+    b = gate.tile([P, HALF_TILES], F32, name="b_" + name)
+    a = gate.tile([P, HALF_TILES], F32, name="a_" + name)
+    one_plus_b = gate.tile([P, HALF_TILES], F32, name="one_plus_b_" + name)
     gp_affine(nc, b[:], total, -2.0 / m, 1.0)
     gp_affine(nc, a[:], b[:], 1.0, 1.0)
     for step in range(SERIES_STEPS):
@@ -114,37 +110,40 @@ def inverse_series(nc, gate, total, m, name):
     return a
 
 
-def gate_weights(nc, gate, sums):
+def gate_weights(nc, gate, sums, half):
+    cols = slice(half * HALF_TILES, (half + 1) * HALF_TILES)
+    tag = "_%d" % half
+
     def new(name):
-        return gate.tile([P, TILES], F32, name=name)
+        return gate.tile([P, HALF_TILES], F32, name=name + tag)
 
     recip1, recip2, recip4, recip8 = new("recip1"), new("recip2"), new("recip4"), new("recip8")
-    nc.vector.reciprocal(out=recip1[:], in_=sums["e1"][:])
+    nc.vector.reciprocal(out=recip1[:], in_=sums["e1"][:, cols])
     gp_mul(nc, recip2[:], recip1[:], recip1[:])
     gp_mul(nc, recip4[:], recip2[:], recip2[:])
     gp_mul(nc, recip8[:], recip4[:], recip4[:])
 
     total0, inv0, scale1 = new("total0"), new("inv0"), new("scale1")
-    gp_mul(nc, total0[:], sums["e2"][:], recip2[:])
+    gp_mul(nc, total0[:], sums["e2"][:, cols], recip2[:])
     gp_affine(nc, total0[:], total0[:], 1.0, TAU**2)
     m0 = 2.0 + TAU**2
-    a0 = inverse_series(nc, gate, total0[:], m0, "0")
+    a0 = inverse_series(nc, gate, total0[:], m0, "0" + tag)
     gp_affine(nc, inv0[:], a0[:], 2.0 / m0, 0.0)
     gp_mul(nc, scale1[:], inv0[:], inv0[:])
 
     total1, scale2 = new("total1"), new("scale2")
-    gp_mul(nc, total1[:], sums["e4"][:], recip4[:])
+    gp_mul(nc, total1[:], sums["e4"][:, cols], recip4[:])
     gp_affine(nc, total1[:], total1[:], 1.0, TAU**4)
     gp_mul(nc, total1[:], total1[:], scale1[:])
-    a1 = inverse_series(nc, gate, total1[:], 2.0, "1")
+    a1 = inverse_series(nc, gate, total1[:], 2.0, "1" + tag)
     gp_mul(nc, scale2[:], scale1[:], a1[:])
     gp_mul(nc, scale2[:], scale2[:], scale2[:])
 
     total2, cond, alpha = new("total2"), new("cond"), new("alpha")
-    gp_mul(nc, total2[:], sums["e8"][:], recip8[:])
+    gp_mul(nc, total2[:], sums["e8"][:, cols], recip8[:])
     gp_affine(nc, total2[:], total2[:], 1.0, TAU**8)
     gp_mul(nc, total2[:], total2[:], scale2[:])
-    a2 = inverse_series(nc, gate, total2[:], 2.0, "2")
+    a2 = inverse_series(nc, gate, total2[:], 2.0, "2" + tag)
     gp_mul(nc, cond[:], scale2[:], a2[:])
     gp_affine(nc, cond[:], cond[:], TAU**8, 0.0)
 
@@ -164,7 +163,6 @@ def tile_combnethe_pa_t_kernel(tc, x, W1o, b1o, W2o, b2o, W1f, b1f, W2f, b2f, ou
         gate = pools.enter_context(tc.tile_pool(name="gate", bufs=1))
         two = pools.enter_context(tc.tile_pool(name="two", bufs=2))
         three = pools.enter_context(tc.tile_pool(name="three", bufs=3))
-        lagged = pools.enter_context(tc.tile_pool(name="lagged", bufs=3 + BLEND_LAG))
         psum_x = pools.enter_context(tc.psum_pool(name="psum_x", bufs=2))
         psum_z = pools.enter_context(tc.psum_pool(name="psum_z", bufs=4))
         psum_l = pools.enter_context(tc.psum_pool(name="psum_l", bufs=2))
@@ -172,16 +170,17 @@ def tile_combnethe_pa_t_kernel(tc, x, W1o, b1o, W2o, b2o, W1f, b1f, W2f, b2f, ou
         identity = keep.tile([P, P], F32, name="identity")
         make_identity(nc, identity[:])
         nets = [
-            stage_network(nc, keep, "o", nc.vector, W1o, b1o, W2o, b2o),
-            stage_network(nc, keep, "f", nc.gpsimd, W1f, b1f, W2f, b2f),
+            load_network(nc, keep, "o", W1o, b1o, W2o, b2o),
+            load_network(nc, keep, "f", W1f, b1f, W2f, b2f),
         ]
+        lay_out_network(nets[0], lambda out, in_: nc.vector.tensor_copy(out=out, in_=in_))
         quantise_network(nc, nets[0])
 
         sums = {}
         for power in ("e1", "e2", "e4", "e8"):
             sums[power] = gate.tile([P, TILES], F32, name="sum_" + power)
+        cond, alpha = [], []
         x_sb, x_t, x_grouped, x_q = {}, {}, {}, {}
-        gate_out = {}
         planes, z_left, h_grouped, h_q, acc, logits, neg_max, e, e_sum, beta = {}, {}, {}, {}, {}, {}, {}, {}, {}, {}
 
         def load_x(g):
@@ -229,7 +228,7 @@ def tile_combnethe_pa_t_kernel(tc, x, W1o, b1o, W2o, b2o, W1f, b1f, W2f, b2f, ou
                 z = psum_z.tile([P, GROUP_ROWS], F32, name="z")
                 cols = slice(t * P, (t + 1) * P)
                 mx_pass(nc, z[:], (codes[:, cols], scales[:, cols]), (rows[0][:], rows[1][:]))
-                if t == PACK - 1 and s < GROUPS and s % 2 == 1:
+                if t == PACK - 1 and s < GROUPS:
                     z_left[s] = z
                 else:
                     nc.scalar.activation(
@@ -287,8 +286,8 @@ def tile_combnethe_pa_t_kernel(tc, x, W1o, b1o, W2o, b2o, W1f, b1f, W2f, b2f, ou
                 e[s] = keep.tile([P, GROUP_TILES, CLASSES], F32, name="e_o_%d" % s)
                 e_sum[s] = sums["e1"][:, s * GROUP_TILES : (s + 1) * GROUP_TILES]
             else:
-                e[s] = lagged.tile([P, GROUP_TILES, CLASSES], F32, name="e_f")
-                e_sum[s] = lagged.tile([P, GROUP_TILES], F32, name="sum_f")
+                e[s] = three.tile([P, GROUP_TILES, CLASSES], F32, name="e_f")
+                e_sum[s] = three.tile([P, GROUP_TILES], F32, name="sum_f")
             for j in range(GROUP_TILES):
                 nc.scalar.activation(
                     out=e[s][:, j, :],
@@ -310,15 +309,20 @@ def tile_combnethe_pa_t_kernel(tc, x, W1o, b1o, W2o, b2o, W1f, b1f, W2f, b2f, ou
                         accum_out=sums[power][:, s * GROUP_TILES + j : s * GROUP_TILES + j + 1],
                     )
 
+        def gate_half(half):
+            cond_half, alpha_half = gate_weights(nc, gate, sums, half)
+            cond.append(cond_half)
+            alpha.append(alpha_half)
+
         def blend_scale_o(s):
             g = s - GROUPS
             for j in range(GROUP_TILES):
-                column = g * GROUP_TILES + j
+                column = (g % HALF_GROUPS) * GROUP_TILES + j
                 nc.scalar.activation(
                     out=e[g][:, j, :],
                     in_=e[g][:, j, :],
                     func=ACT.Copy,
-                    scale=gate_out["alpha"][:, column : column + 1],
+                    scale=alpha[g // HALF_GROUPS][:, column : column + 1],
                 )
 
         def blend_reciprocal(s):
@@ -327,10 +331,11 @@ def tile_combnethe_pa_t_kernel(tc, x, W1o, b1o, W2o, b2o, W1f, b1f, W2f, b2f, ou
 
         def blend_beta(s):
             g = s - GROUPS
+            member = g % HALF_GROUPS
             nc.vector.tensor_mul(
                 out=beta[s][:],
                 in0=beta[s][:],
-                in1=gate_out["cond"][:, g * GROUP_TILES : (g + 1) * GROUP_TILES],
+                in1=cond[g // HALF_GROUPS][:, member * GROUP_TILES : (member + 1) * GROUP_TILES],
             )
 
         def blend_and_store(s):
@@ -350,13 +355,12 @@ def tile_combnethe_pa_t_kernel(tc, x, W1o, b1o, W2o, b2o, W1f, b1f, W2f, b2f, ou
             if first <= index < last:
                 stage(index)
 
-        for i in range(-4, STEPS + BLEND_LAG + 4):
-            blended = i - 3 - BLEND_LAG
+        for i in range(-4, STEPS + 4):
             run(load_x, i + 4, 0, GROUPS)
             run(hidden_layer, i + 1, 0, STEPS)
             run(regroup_h, i, 0, STEPS)
             run(lambda g: copy_x_out(g, 0), i + 2, 0, GROUPS)
-            run(blend_reciprocal, blended, GROUPS, STEPS)
+            run(blend_reciprocal, i - 3, GROUPS, STEPS)
             run(quantise_h, i, 0, STEPS)
             run(lambda g: copy_x_out(g, 1), i + 2, 0, GROUPS)
             run(vector_relu, i + 1, 0, GROUPS)
@@ -364,13 +368,15 @@ def tile_combnethe_pa_t_kernel(tc, x, W1o, b1o, W2o, b2o, W1f, b1f, W2f, b2f, ou
             run(head, i, 0, STEPS)
             run(add_bias, i - 1, 0, STEPS)
             run(quantise_x, i + 2, 0, GROUPS)
-            run(blend_beta, blended, GROUPS, STEPS)
+            run(blend_beta, i - 3, GROUPS, STEPS)
             run(row_max, i - 1, 0, STEPS)
+            run(blend_scale_o, i - 2, GROUPS, STEPS)
             run(exponentials, i - 2, 0, STEPS)
             run(power_sums, i - 2, 0, GROUPS)
-            run(blend_scale_o, blended + 1, GROUPS, STEPS)
-            run(blend_and_store, blended, GROUPS, STEPS)
-            if i == 0:
+            run(blend_and_store, i - 3, GROUPS, STEPS)
+            if i == -1:
+                lay_out_network(nets[1], lambda out, in_: nc.scalar.copy(out=out, in_=in_))
+            if i == 2:
                 quantise_network(nc, nets[1])
-            if i - 3 == GROUPS - 1:
-                gate_out["cond"], gate_out["alpha"] = gate_weights(nc, gate, sums)
+            if i - 3 in (HALF_GROUPS - 1, GROUPS - 1):
+                gate_half((i - 3) // HALF_GROUPS)

from contextlib import ExitStack

import concourse.mybir as mybir
from concourse.masks import make_identity

F32 = mybir.dt.float32
BF16 = mybir.dt.bfloat16
U32 = mybir.dt.uint32
U8 = mybir.dt.uint8
FP8X4 = mybir.dt.float8_e4m3fn_x4
ACT = mybir.ActivationFunctionType
ALU = mybir.AluOpType
AXIS = mybir.AxisListType

P = 128
PACK = 4
ROWS, D_IN, D_H, CLASSES = 8192, 512, 512, 128
TILES = ROWS // P
GROUP_TILES = 4
GROUP_ROWS = GROUP_TILES * P
GROUPS = TILES // GROUP_TILES
STEPS = 2 * GROUPS
HALF_GROUPS = GROUPS // 2
HALF_TILES = TILES // 2
WORDS = D_IN // 2
TAU = 0.5
SERIES_STEPS = 3

FLOPS = 2 * (2 * ROWS * D_IN * D_H + 2 * ROWS * D_H * CLASSES)


def quantise(nc, grouped, codes, scales):
    nc.vector.quantize_mx(out=codes.bitcast(FP8X4), scales=scales, in_=grouped)


def mx_pass(nc, acc, stationary, moving):
    nc.tensor.matmul_mx(
        out=acc,
        lhsT=stationary[0].bitcast(FP8X4),
        lhsT_scale=stationary[1],
        rhs=moving[0].bitcast(FP8X4),
        rhs_scale=moving[1],
        start=True,
        stop=True,
    )


def load_network(nc, keep, net, w1, b1, w2, b2):
    tiles = {
        "w1_raw": keep.tile([P, PACK, D_H], BF16, name="w1_raw_" + net),
        "w1_grouped": keep.tile([P, D_H, PACK], BF16, name="w1_grouped_" + net, align_bytes=64),
        "w1": (
            keep.tile([P, D_H], U32, name="w1_codes_" + net, align_bytes=64),
            keep.tile([P, D_H], U8, name="w1_scales_" + net, align_bytes=64),
        ),
        "b1_raw": keep.tile([P, PACK], BF16, name="b1_raw_" + net),
        "b1": keep.tile([P, PACK], F32, name="b1_cols_" + net),
        "w2_raw": keep.tile([P, PACK, CLASSES], BF16, name="w2_raw_" + net),
        "w2_grouped": keep.tile([P, CLASSES, PACK], BF16, name="w2_grouped_" + net, align_bytes=64),
        "w2": (
            keep.tile([P, CLASSES], U32, name="w2_codes_" + net, align_bytes=64),
            keep.tile([P, CLASSES], U8, name="w2_scales_" + net, align_bytes=64),
        ),
        "b2_raw": keep.tile([P, CLASSES], BF16, name="b2_raw_" + net),
        "b2": keep.tile([P, CLASSES], F32, name="b2_rows_" + net),
    }
    nc.scalar.dma_start(
        out=tiles["w1_raw"][:].rearrange("p (u e) h -> p u e h", u=2),
        in_=w1.rearrange("(u p e) h -> p u e h", u=2, e=2),
    )
    nc.scalar.dma_start(out=tiles["b1_raw"][:], in_=b1.rearrange("(p t) -> p t", t=PACK))
    nc.scalar.dma_start(out=tiles["w2_raw"][:], in_=w2.rearrange("(p t) c -> p t c", t=PACK))
    nc.scalar.dma_start(out=tiles["b2_raw"][:], in_=b2.partition_broadcast(P))
    return tiles


def lay_out_network(net, copy):
    copy(
        net["w1_grouped"][:].rearrange("p (t m) j -> p t m j", t=PACK),
        net["w1_raw"][:].rearrange("p j (m t) -> p t m j", t=PACK),
    )
    copy(net["b1"][:], net["b1_raw"][:])
    copy(net["w2_grouped"][:], net["w2_raw"][:].rearrange("p t c -> p c t"))
    copy(net["b2"][:], net["b2_raw"][:])


def quantise_network(nc, net):
    quantise(nc, net["w1_grouped"][:].rearrange("p c j -> p (c j)"), net["w1"][0][:], net["w1"][1][:])
    quantise(nc, net["w2_grouped"][:].rearrange("p c t -> p (c t)"), net["w2"][0][:], net["w2"][1][:])


def gp_affine(nc, out, in_, mul, add):
    nc.gpsimd.tensor_scalar(out=out, in0=in_, scalar1=mul, scalar2=add, op0=ALU.mult, op1=ALU.add)


def gp_mul(nc, out, in0, in1):
    nc.gpsimd.tensor_tensor(out=out, in0=in0, in1=in1, op=ALU.mult)


def inverse_series(nc, gate, total, m, name):
    b = gate.tile([P, HALF_TILES], F32, name="b_" + name)
    a = gate.tile([P, HALF_TILES], F32, name="a_" + name)
    one_plus_b = gate.tile([P, HALF_TILES], F32, name="one_plus_b_" + name)
    gp_affine(nc, b[:], total, -2.0 / m, 1.0)
    gp_affine(nc, a[:], b[:], 1.0, 1.0)
    for step in range(SERIES_STEPS):
        gp_mul(nc, b[:], b[:], b[:])
        gp_affine(nc, one_plus_b[:], b[:], 1.0, 1.0)
        gp_mul(nc, a[:], a[:], one_plus_b[:])
    return a


def gate_weights(nc, gate, sums, half):
    cols = slice(half * HALF_TILES, (half + 1) * HALF_TILES)
    tag = "_%d" % half

    def new(name):
        return gate.tile([P, HALF_TILES], F32, name=name + tag)

    recip1, recip2, recip4, recip8 = new("recip1"), new("recip2"), new("recip4"), new("recip8")
    nc.vector.reciprocal(out=recip1[:], in_=sums["e1"][:, cols])
    gp_mul(nc, recip2[:], recip1[:], recip1[:])
    gp_mul(nc, recip4[:], recip2[:], recip2[:])
    gp_mul(nc, recip8[:], recip4[:], recip4[:])

    total0, inv0, scale1 = new("total0"), new("inv0"), new("scale1")
    gp_mul(nc, total0[:], sums["e2"][:, cols], recip2[:])
    gp_affine(nc, total0[:], total0[:], 1.0, TAU**2)
    m0 = 2.0 + TAU**2
    a0 = inverse_series(nc, gate, total0[:], m0, "0" + tag)
    gp_affine(nc, inv0[:], a0[:], 2.0 / m0, 0.0)
    gp_mul(nc, scale1[:], inv0[:], inv0[:])

    total1, scale2 = new("total1"), new("scale2")
    gp_mul(nc, total1[:], sums["e4"][:, cols], recip4[:])
    gp_affine(nc, total1[:], total1[:], 1.0, TAU**4)
    gp_mul(nc, total1[:], total1[:], scale1[:])
    a1 = inverse_series(nc, gate, total1[:], 2.0, "1" + tag)
    gp_mul(nc, scale2[:], scale1[:], a1[:])
    gp_mul(nc, scale2[:], scale2[:], scale2[:])

    total2, cond, alpha = new("total2"), new("cond"), new("alpha")
    gp_mul(nc, total2[:], sums["e8"][:, cols], recip8[:])
    gp_affine(nc, total2[:], total2[:], 1.0, TAU**8)
    gp_mul(nc, total2[:], total2[:], scale2[:])
    a2 = inverse_series(nc, gate, total2[:], 2.0, "2" + tag)
    gp_mul(nc, cond[:], scale2[:], a2[:])
    gp_affine(nc, cond[:], cond[:], TAU**8, 0.0)

    gp_affine(nc, alpha[:], cond[:], -1.0, 1.0)
    gp_mul(nc, alpha[:], alpha[:], recip1[:])
    return cond, alpha


def tile_combnethe_pa_t_kernel(tc, x, W1o, b1o, W2o, b2o, W1f, b1f, W2f, b2f, out):
    nc = tc.nc
    x_rows = x.rearrange("(p j) k -> p j k", j=TILES)
    out_rows = out.rearrange("(p j) c -> p j c", j=TILES)

    with ExitStack() as pools:
        pools.enter_context(tc.manual_schedule())
        keep = pools.enter_context(tc.tile_pool(name="keep", bufs=1))
        gate = pools.enter_context(tc.tile_pool(name="gate", bufs=1))
        two = pools.enter_context(tc.tile_pool(name="two", bufs=2))
        three = pools.enter_context(tc.tile_pool(name="three", bufs=3))
        psum_x = pools.enter_context(tc.psum_pool(name="psum_x", bufs=2))
        psum_z = pools.enter_context(tc.psum_pool(name="psum_z", bufs=4))
        psum_l = pools.enter_context(tc.psum_pool(name="psum_l", bufs=2))

        identity = keep.tile([P, P], F32, name="identity")
        make_identity(nc, identity[:])
        nets = [
            load_network(nc, keep, "o", W1o, b1o, W2o, b2o),
            load_network(nc, keep, "f", W1f, b1f, W2f, b2f),
        ]
        lay_out_network(nets[0], lambda out, in_: nc.vector.tensor_copy(out=out, in_=in_))
        quantise_network(nc, nets[0])

        sums = {}
        for power in ("e1", "e2", "e4", "e8"):
            sums[power] = gate.tile([P, TILES], F32, name="sum_" + power)
        cond, alpha = [], []
        x_sb, x_t, x_grouped, x_q = {}, {}, {}, {}
        planes, z_left, h_grouped, h_q, acc, logits, neg_max, e, e_sum, beta = {}, {}, {}, {}, {}, {}, {}, {}, {}, {}

        def load_x(g):
            x_sb[g] = three.tile([P, GROUP_TILES * D_IN], BF16, name="x_sb")
            nc.sync.dma_start(
                out=x_sb[g][:].rearrange("p (j k) -> p j k", j=GROUP_TILES),
                in_=x_rows[:, g * GROUP_TILES : (g + 1) * GROUP_TILES, :],
            )

        def transpose_x(g):
            x_words = x_sb[g][:].bitcast(F32)
            x_t[g] = []
            for half in range(2):
                bank = psum_x.tile([P, 2, 2, P], F32, name="x_t")
                for jj in range(2):
                    for u in range(2):
                        first = (2 * half + jj) * WORDS + u * P
                        nc.tensor.transpose(bank[:, jj, u, :], x_words[:, first : first + P], identity[:])
                x_t[g].append(bank)

        def copy_x_out(g, half):
            if half == 0:
                x_grouped[g] = two.tile([P, GROUP_ROWS * PACK], BF16, name="x_grouped", align_bytes=64)
            grouped_words = x_grouped[g][:].bitcast(F32)
            nc.vector.tensor_copy(
                out=grouped_words[:, half * 2 * WORDS : (half + 1) * 2 * WORDS].rearrange(
                    "p (j r u) -> p j r u", j=2, u=2
                ),
                in_=x_t[g][half][:].rearrange("p j u r -> p j r u"),
            )

        def quantise_x(g):
            x_q[g] = (
                keep.tile([P, GROUP_ROWS], U32, name="x_codes_%d" % g, align_bytes=64),
                keep.tile([P, GROUP_ROWS], U8, name="x_scales_%d" % g, align_bytes=64),
            )
            quantise(nc, x_grouped[g][:], x_q[g][0][:], x_q[g][1][:])

        def hidden_layer(s):
            net = nets[s // GROUPS]
            codes, scales = net["w1"]
            rows = x_q[s % GROUPS]
            planes[s] = two.tile([P, PACK, GROUP_ROWS], BF16, name="planes")
            for t in range(PACK):
                z = psum_z.tile([P, GROUP_ROWS], F32, name="z")
                cols = slice(t * P, (t + 1) * P)
                mx_pass(nc, z[:], (codes[:, cols], scales[:, cols]), (rows[0][:], rows[1][:]))
                if t == PACK - 1 and s < GROUPS:
                    z_left[s] = z
                else:
                    nc.scalar.activation(
                        out=planes[s][:, t, :], in_=z[:], func=ACT.Relu, bias=net["b1"][:, t : t + 1], scale=1.0
                    )

        def vector_relu(s):
            if s in z_left:
                t = PACK - 1
                nc.vector.tensor_scalar(
                    out=planes[s][:, t, :],
                    in0=z_left[s][:],
                    scalar1=nets[s // GROUPS]["b1"][:, t : t + 1],
                    scalar2=0.0,
                    op0=ALU.add,
                    op1=ALU.max,
                )

        def regroup_h(s):
            h_grouped[s] = two.tile([P, GROUP_ROWS, PACK], BF16, name="h_grouped", align_bytes=64)
            nc.vector.tensor_copy(
                out=h_grouped[s][:].rearrange("p (c i) t -> p c t i", i=4),
                in_=planes[s][:].rearrange("p t (c i) -> p c t i", i=4),
            )

        def quantise_h(s):
            h_q[s] = (
                two.tile([P, GROUP_ROWS], U32, name="h_codes", align_bytes=64),
                two.tile([P, GROUP_ROWS], U8, name="h_scales", align_bytes=64),
            )
            quantise(nc, h_grouped[s][:].rearrange("p r t -> p (r t)"), h_q[s][0][:], h_q[s][1][:])

        def head(s):
            w2 = nets[s // GROUPS]["w2"]
            acc[s] = psum_l.tile([P, GROUP_TILES, CLASSES], F32, name="acc")
            for j in range(GROUP_TILES):
                cols = slice(j * P, (j + 1) * P)
                mx_pass(nc, acc[s][:, j, :], (h_q[s][0][:, cols], h_q[s][1][:, cols]), (w2[0][:], w2[1][:]))

        def add_bias(s):
            logits[s] = three.tile([P, GROUP_TILES, CLASSES], F32, name="logits")
            nc.vector.tensor_tensor(
                out=logits[s][:],
                in0=acc[s][:],
                in1=nets[s // GROUPS]["b2"][:].unsqueeze(1).to_broadcast([P, GROUP_TILES, CLASSES]),
                op=ALU.add,
            )

        def row_max(s):
            neg_max[s] = three.tile([P, GROUP_TILES], F32, name="neg_max")
            nc.vector.tensor_reduce(out=neg_max[s][:], in_=logits[s][:], axis=AXIS.X, op=ALU.max, negate=True)

        def exponentials(s):
            if s < GROUPS:
                e[s] = keep.tile([P, GROUP_TILES, CLASSES], F32, name="e_o_%d" % s)
                e_sum[s] = sums["e1"][:, s * GROUP_TILES : (s + 1) * GROUP_TILES]
            else:
                e[s] = three.tile([P, GROUP_TILES, CLASSES], F32, name="e_f")
                e_sum[s] = three.tile([P, GROUP_TILES], F32, name="sum_f")
            for j in range(GROUP_TILES):
                nc.scalar.activation(
                    out=e[s][:, j, :],
                    in_=logits[s][:, j, :],
                    func=ACT.Exp,
                    bias=neg_max[s][:, j : j + 1],
                    scale=1.0,
                    accum_out=e_sum[s][:, j : j + 1],
                )

        def power_sums(s):
            powers = two.tile([P, GROUP_TILES, CLASSES], F32, name="powers")
            for power in ("e2", "e4", "e8"):
                for j in range(GROUP_TILES):
                    nc.scalar.activation(
                        out=powers[:, j, :],
                        in_=e[s][:, j, :] if power == "e2" else powers[:, j, :],
                        func=ACT.Square,
                        accum_out=sums[power][:, s * GROUP_TILES + j : s * GROUP_TILES + j + 1],
                    )

        def gate_half(half):
            cond_half, alpha_half = gate_weights(nc, gate, sums, half)
            cond.append(cond_half)
            alpha.append(alpha_half)

        def blend_scale_o(s):
            g = s - GROUPS
            for j in range(GROUP_TILES):
                column = (g % HALF_GROUPS) * GROUP_TILES + j
                nc.scalar.activation(
                    out=e[g][:, j, :],
                    in_=e[g][:, j, :],
                    func=ACT.Copy,
                    scale=alpha[g // HALF_GROUPS][:, column : column + 1],
                )

        def blend_reciprocal(s):
            beta[s] = three.tile([P, GROUP_TILES], F32, name="beta")
            nc.vector.reciprocal(out=beta[s][:], in_=e_sum[s][:])

        def blend_beta(s):
            g = s - GROUPS
            member = g % HALF_GROUPS
            nc.vector.tensor_mul(
                out=beta[s][:],
                in0=beta[s][:],
                in1=cond[g // HALF_GROUPS][:, member * GROUP_TILES : (member + 1) * GROUP_TILES],
            )

        def blend_and_store(s):
            g = s - GROUPS
            for j in range(GROUP_TILES):
                nc.vector.scalar_tensor_tensor(
                    out=e[s][:, j, :],
                    in0=e[s][:, j, :],
                    scalar=beta[s][:, j : j + 1],
                    in1=e[g][:, j, :],
                    op0=ALU.mult,
                    op1=ALU.add,
                )
            nc.sync.dma_start(out=out_rows[:, g * GROUP_TILES : (g + 1) * GROUP_TILES, :], in_=e[s][:])

        def run(stage, index, first, last):
            if first <= index < last:
                stage(index)

        for i in range(-4, STEPS + 4):
            run(load_x, i + 4, 0, GROUPS)
            run(hidden_layer, i + 1, 0, STEPS)
            run(regroup_h, i, 0, STEPS)
            run(lambda g: copy_x_out(g, 0), i + 2, 0, GROUPS)
            run(blend_reciprocal, i - 3, GROUPS, STEPS)
            run(quantise_h, i, 0, STEPS)
            run(lambda g: copy_x_out(g, 1), i + 2, 0, GROUPS)
            run(vector_relu, i + 1, 0, GROUPS)
            run(transpose_x, i + 3, 0, GROUPS)
            run(head, i, 0, STEPS)
            run(add_bias, i - 1, 0, STEPS)
            run(quantise_x, i + 2, 0, GROUPS)
            run(blend_beta, i - 3, GROUPS, STEPS)
            run(row_max, i - 1, 0, STEPS)
            run(blend_scale_o, i - 2, GROUPS, STEPS)
            run(exponentials, i - 2, 0, STEPS)
            run(power_sums, i - 2, 0, GROUPS)
            run(blend_and_store, i - 3, GROUPS, STEPS)
            if i == -1:
                lay_out_network(nets[1], lambda out, in_: nc.scalar.copy(out=out, in_=in_))
            if i == 2:
                quantise_network(nc, nets[1])
            if i - 3 in (HALF_GROUPS - 1, GROUPS - 1):
                gate_half((i - 3) // HALF_GROUPS)
